import numpy as np
import ml_dtypes

BF16 = ml_dtypes.bfloat16


def bf(x):
    return np.asarray(x, np.float32).astype(BF16)


def f32(x):
    return np.asarray(x, np.float32)


def f64(x):
    return np.asarray(x).astype(np.float64)


def striped(idx):
    return np.tile(idx.reshape(-1, 16).T, (8, 1))


D, C, S, N = 128, 256, 512, 128
GAMMA = 12.0
RANGE = 0.028
PI = 3.141592653589793
SPAN = 0.95
ENT_SCALE = 0.1


def setup_inputs():
    return {"ent": f32(ENT_SCALE * np.random.standard_normal((C, S))), "rel": f32(SPAN * RANGE * np.random.uniform(-1.0, 1.0, (D, N))), "offs": striped(np.random.permutation(np.tile(np.arange(S), 2))[:N])}


def reference(ent, rel, offs):
    idx = offs[:16].T.reshape(-1)
    e = f64(ent)
    re_t, im_t = e[:D], e[D:]
    phase = f64(rel) / (RANGE / PI)
    re_r, im_r = np.cos(phase), np.sin(phase)
    re_h, im_h = re_t[:, idx], im_t[:, idx]
    re_rot = re_h * re_r - im_h * im_r
    im_rot = re_h * im_r + im_h * re_r
    re_diff = re_rot[:, :, None] - re_t[:, None, :]
    im_diff = im_rot[:, :, None] - im_t[:, None, :]
    return GAMMA - np.sqrt(re_diff ** 2 + im_diff ** 2).sum(axis=0)

@@ -1,0 +1,82 @@
+import math
+
+import concourse.mybir as mybir
+
+F32 = mybir.dt.float32
+BF16 = mybir.dt.bfloat16
+U16 = mybir.dt.uint16
+ALU = mybir.AluOpType
+FUNC = mybir.ActivationFunctionType
+
+D = 128
+S = 512
+N = 128
+GAMMA = 12.0
+PHASE_PER_REL = math.pi / 0.028
+
+FLOPS = 2 * D * N * S
+
+
+def tile_rotate_kernel(tc, ent, rel, offs, out):
+    nc = tc.nc
+    with (
+        tc.tile_pool(name="held", bufs=1) as held,
+        tc.tile_pool(name="work", bufs=3) as work,
+        tc.psum_pool(name="psum", bufs=1) as psum,
+    ):
+        offsets = held.tile([128, N // 16], U16, name="offsets")
+        nc.sync.dma_start(offsets[:], offs)
+        rel_sb = held.tile([D, N], F32, name="rel_sb")
+        nc.gpsimd.dma_start(rel_sb[:], rel)
+        re_ent = held.tile([D, S], F32, name="re_ent")
+        nc.sync.dma_start(re_ent[:], ent[0:D, :])
+        im_ent = held.tile([D, S], F32, name="im_ent")
+        nc.scalar.dma_start(im_ent[:], ent[D : 2 * D, :])
+
+        pick_row = held.tile([D, 2 * N - 1], BF16, name="pick_row")
+        nc.gpsimd.memset(pick_row[:], 0.0)
+        nc.gpsimd.memset(pick_row[:, N - 1 : N], 1.0)
+
+        half_pi = held.tile([D, 1], F32, name="half_pi")
+        nc.vector.memset(half_pi[:], math.pi / 2)
+        sin_ph = held.tile([D, N], F32, name="sin_ph")
+        nc.scalar.activation(sin_ph[:], rel_sb[:], FUNC.Sin, scale=PHASE_PER_REL)
+        abs_rel = held.tile([D, N], F32, name="abs_rel")
+        nc.scalar.activation(abs_rel[:], rel_sb[:], FUNC.Abs)
+        cos_ph = held.tile([D, N], F32, name="cos_ph")
+        nc.scalar.activation(cos_ph[:], abs_rel[:], FUNC.Sin, bias=half_pi[:], scale=-PHASE_PER_REL)
+
+        re_cos = held.tile([D, N], F32, name="re_cos")
+        nc.vector.tensor_tensor(re_cos[:], re_ent[:].indirect(offsets[:]), cos_ph[:], ALU.mult)
+        im_sin = held.tile([D, N], F32, name="im_sin")
+        nc.vector.tensor_tensor(im_sin[:], im_ent[:].indirect(offsets[:]), sin_ph[:], ALU.mult)
+        re_sin = held.tile([D, N], F32, name="re_sin")
+        nc.vector.tensor_tensor(re_sin[:], re_ent[:].indirect(offsets[:]), sin_ph[:], ALU.mult)
+        im_cos = held.tile([D, N], F32, name="im_cos")
+        nc.vector.tensor_tensor(im_cos[:], im_ent[:].indirect(offsets[:]), cos_ph[:], ALU.mult)
+        re_rot = held.tile([D, N], F32, name="re_rot")
+        nc.vector.tensor_tensor(re_rot[:], re_cos[:], im_sin[:], ALU.subtract)
+        im_rot = held.tile([D, N], F32, name="im_rot")
+        nc.vector.tensor_tensor(im_rot[:], re_sin[:], im_cos[:], ALU.add)
+
+        dist_sum = psum.tile([N, S], F32, name="dist_sum")
+        for j in range(N):
+            re_sq = work.tile([D, S], F32, name="re_sq")
+            nc.scalar.activation(re_sq[:], re_ent[:], FUNC.Square, bias=re_rot[:, j : j + 1], scale=-1.0)
+            im_sq = work.tile([D, S], F32, name="im_sq")
+            nc.scalar.activation(im_sq[:], im_ent[:], FUNC.Square, bias=im_rot[:, j : j + 1], scale=-1.0)
+            mod_sq = work.tile([D, S], F32, name="mod_sq")
+            nc.vector.tensor_tensor(mod_sq[:], re_sq[:], im_sq[:], ALU.add)
+            modulus = work.tile([D, S], BF16, name="modulus")
+            nc.scalar.activation(modulus[:], mod_sq[:], FUNC.Sqrt)
+            nc.tensor.matmul(
+                dist_sum[:],
+                pick_row[:, N - 1 - j : 2 * N - 1 - j],
+                modulus[:],
+                start=(j == 0),
+                stop=(j == N - 1),
+            )
+
+        score = held.tile([N, S], F32, name="score")
+        nc.vector.tensor_scalar(score[:], dist_sum[:], -1.0, GAMMA, ALU.mult, ALU.add)
+        nc.sync.dma_start(out, score[:])

@@ -14,6 +14,8 @@ N = 128
 GAMMA = 12.0
 PHASE_PER_REL = math.pi / 0.028
 
+GUARD = 1.0 + 2.0**-20
+
 FLOPS = 2 * D * N * S
 
 
@@ -46,6 +48,14 @@ def tile_rotate_kernel(tc, ent, rel, offs, out):
         cos_ph = held.tile([D, N], F32, name="cos_ph")
         nc.scalar.activation(cos_ph[:], abs_rel[:], FUNC.Sin, bias=half_pi[:], scale=-PHASE_PER_REL)
 
+        re_ent_sq = held.tile([D, S], F32, name="re_ent_sq")
+        nc.vector.tensor_tensor(re_ent_sq[:], re_ent[:], re_ent[:], ALU.mult)
+        im_ent_sq = held.tile([D, S], F32, name="im_ent_sq")
+        nc.vector.tensor_tensor(im_ent_sq[:], im_ent[:], im_ent[:], ALU.mult)
+        ent_norm = held.tile([D, S], F32, name="ent_norm")
+        nc.vector.tensor_tensor(ent_norm[:], re_ent_sq[:], im_ent_sq[:], ALU.add)
+        nc.vector.tensor_scalar(ent_norm[:], ent_norm[:], GUARD, None, ALU.mult)
+
         re_cos = held.tile([D, N], F32, name="re_cos")
         nc.vector.tensor_tensor(re_cos[:], re_ent[:].indirect(offsets[:]), cos_ph[:], ALU.mult)
         im_sin = held.tile([D, N], F32, name="im_sin")
@@ -59,16 +69,30 @@ def tile_rotate_kernel(tc, ent, rel, offs, out):
         im_rot = held.tile([D, N], F32, name="im_rot")
         nc.vector.tensor_tensor(im_rot[:], re_sin[:], im_cos[:], ALU.add)
 
+        re_coef = held.tile([D, N], F32, name="re_coef")
+        nc.vector.tensor_scalar(re_coef[:], re_rot[:], -2.0, None, ALU.mult)
+        im_coef = held.tile([D, N], F32, name="im_coef")
+        nc.vector.tensor_scalar(im_coef[:], im_rot[:], -2.0, None, ALU.mult)
+        re_rot_sq = held.tile([D, N], F32, name="re_rot_sq")
+        nc.vector.tensor_tensor(re_rot_sq[:], re_rot[:], re_rot[:], ALU.mult)
+        im_rot_sq = held.tile([D, N], F32, name="im_rot_sq")
+        nc.vector.tensor_tensor(im_rot_sq[:], im_rot[:], im_rot[:], ALU.mult)
+        rot_norm = held.tile([D, N], F32, name="rot_norm")
+        nc.vector.tensor_tensor(rot_norm[:], re_rot_sq[:], im_rot_sq[:], ALU.add)
+        nc.vector.tensor_scalar(rot_norm[:], rot_norm[:], GUARD, None, ALU.mult)
+
         dist_sum = psum.tile([N, S], F32, name="dist_sum")
         for j in range(N):
-            re_sq = work.tile([D, S], F32, name="re_sq")
-            nc.scalar.activation(re_sq[:], re_ent[:], FUNC.Square, bias=re_rot[:, j : j + 1], scale=-1.0)
-            im_sq = work.tile([D, S], F32, name="im_sq")
-            nc.scalar.activation(im_sq[:], im_ent[:], FUNC.Square, bias=im_rot[:, j : j + 1], scale=-1.0)
-            mod_sq = work.tile([D, S], F32, name="mod_sq")
-            nc.vector.tensor_tensor(mod_sq[:], re_sq[:], im_sq[:], ALU.add)
+            partial = work.tile([D, S], F32, name="partial")
+            nc.vector.scalar_tensor_tensor(
+                partial[:], re_ent[:], re_coef[:, j : j + 1], ent_norm[:], ALU.mult, ALU.add
+            )
+            cross = work.tile([D, S], F32, name="cross")
+            nc.vector.scalar_tensor_tensor(
+                cross[:], im_ent[:], im_coef[:, j : j + 1], partial[:], ALU.mult, ALU.add
+            )
             modulus = work.tile([D, S], BF16, name="modulus")
-            nc.scalar.activation(modulus[:], mod_sq[:], FUNC.Sqrt)
+            nc.scalar.activation(modulus[:], cross[:], FUNC.Sqrt, bias=rot_norm[:, j : j + 1])
             nc.tensor.matmul(
                 dist_sum[:],
                 pick_row[:, N - 1 - j : 2 * N - 1 - j],

@@ -29,7 +29,7 @@ def tile_rotate_kernel(tc, ent, rel, offs, out):
         offsets = held.tile([128, N // 16], U16, name="offsets")
         nc.sync.dma_start(offsets[:], offs)
         rel_sb = held.tile([D, N], F32, name="rel_sb")
-        nc.gpsimd.dma_start(rel_sb[:], rel)
+        nc.scalar.dma_start(rel_sb[:], rel)
         re_ent = held.tile([D, S], F32, name="re_ent")
         nc.sync.dma_start(re_ent[:], ent[0:D, :])
         im_ent = held.tile([D, S], F32, name="im_ent")
@@ -83,16 +83,25 @@ def tile_rotate_kernel(tc, ent, rel, offs, out):
 
         dist_sum = psum.tile([N, S], F32, name="dist_sum")
         for j in range(N):
-            partial = work.tile([D, S], F32, name="partial")
-            nc.vector.scalar_tensor_tensor(
-                partial[:], re_ent[:], re_coef[:, j : j + 1], ent_norm[:], ALU.mult, ALU.add
-            )
-            cross = work.tile([D, S], F32, name="cross")
-            nc.vector.scalar_tensor_tensor(
-                cross[:], im_ent[:], im_coef[:, j : j + 1], partial[:], ALU.mult, ALU.add
-            )
             modulus = work.tile([D, S], BF16, name="modulus")
-            nc.scalar.activation(modulus[:], cross[:], FUNC.Sqrt, bias=rot_norm[:, j : j + 1])
+            if j % 3 == 0:
+                re_sq = work.tile([D, S], F32, name="re_sq")
+                nc.scalar.activation(re_sq[:], re_ent[:], FUNC.Square, bias=re_rot[:, j : j + 1], scale=-1.0)
+                im_sq = work.tile([D, S], F32, name="im_sq")
+                nc.scalar.activation(im_sq[:], im_ent[:], FUNC.Square, bias=im_rot[:, j : j + 1], scale=-1.0)
+                mod_sq = work.tile([D, S], F32, name="mod_sq")
+                nc.vector.tensor_tensor(mod_sq[:], re_sq[:], im_sq[:], ALU.add)
+                nc.scalar.activation(modulus[:], mod_sq[:], FUNC.Sqrt)
+            else:
+                partial = work.tile([D, S], F32, name="partial")
+                nc.vector.scalar_tensor_tensor(
+                    partial[:], re_ent[:], re_coef[:, j : j + 1], ent_norm[:], ALU.mult, ALU.add
+                )
+                cross = work.tile([D, S], F32, name="cross")
+                nc.vector.scalar_tensor_tensor(
+                    cross[:], im_ent[:], im_coef[:, j : j + 1], partial[:], ALU.mult, ALU.add
+                )
+                nc.scalar.activation(modulus[:], cross[:], FUNC.Sqrt, bias=rot_norm[:, j : j + 1])
             nc.tensor.matmul(
                 dist_sum[:],
                 pick_row[:, N - 1 - j : 2 * N - 1 - j],

@@ -14,9 +14,14 @@ N = 128
 GAMMA = 12.0
 PHASE_PER_REL = math.pi / 0.028
 
-GUARD = 1.0 + 2.0**-20
+PAIRS = [(a, b) for a in range(3) for b in range(3 - a)]
+K = 2 * len(PAIRS) + 3 + 3
 
-FLOPS = 2 * D * N * S
+BLOCKS = ((0, 16), (16, 32), (32, 64), (64, D))
+
+GUARD = 1.0 + 2.0**-18
+
+FLOPS = 7 * D * N * S
 
 
 def tile_rotate_kernel(tc, ent, rel, offs, out):
@@ -24,7 +29,7 @@ def tile_rotate_kernel(tc, ent, rel, offs, out):
     with (
         tc.tile_pool(name="held", bufs=1) as held,
         tc.tile_pool(name="work", bufs=3) as work,
-        tc.psum_pool(name="psum", bufs=1) as psum,
+        tc.psum_pool(name="banks", bufs=4) as banks,
     ):
         offsets = held.tile([128, N // 16], U16, name="offsets")
         nc.sync.dma_start(offsets[:], offs)
@@ -35,26 +40,32 @@ def tile_rotate_kernel(tc, ent, rel, offs, out):
         im_ent = held.tile([D, S], F32, name="im_ent")
         nc.scalar.dma_start(im_ent[:], ent[D : 2 * D, :])
 
-        pick_row = held.tile([D, 2 * N - 1], BF16, name="pick_row")
-        nc.gpsimd.memset(pick_row[:], 0.0)
-        nc.gpsimd.memset(pick_row[:, N - 1 : N], 1.0)
-
+        ones = held.tile([D, S], BF16, name="ones")
+        nc.gpsimd.memset(ones[:], 1.0)
+        dist_sums = [held.tile([N, S], F32, name=f"dist_sum{i}") for i in range(2)]
+        nc.gpsimd.memset(dist_sums[0][:], -GAMMA)
+        nc.gpsimd.memset(dist_sums[1][:], 0.0)
         half_pi = held.tile([D, 1], F32, name="half_pi")
         nc.vector.memset(half_pi[:], math.pi / 2)
+
+        def split(value, name, cast):
+            shape = [D, value.shape[1]]
+            high = held.tile(shape, BF16, name=name + "_high")
+            cast(high[:], value)
+            rest = held.tile(shape, F32, name=name + "_rest")
+            nc.vector.tensor_tensor(rest[:], value, high[:], ALU.subtract)
+            middle = held.tile(shape, BF16, name=name + "_middle")
+            cast(middle[:], rest[:])
+            low = held.tile(shape, BF16, name=name + "_low")
+            nc.vector.tensor_tensor(low[:], rest[:], middle[:], ALU.subtract)
+            return high, middle, low
+
         sin_ph = held.tile([D, N], F32, name="sin_ph")
         nc.scalar.activation(sin_ph[:], rel_sb[:], FUNC.Sin, scale=PHASE_PER_REL)
         abs_rel = held.tile([D, N], F32, name="abs_rel")
         nc.scalar.activation(abs_rel[:], rel_sb[:], FUNC.Abs)
         cos_ph = held.tile([D, N], F32, name="cos_ph")
         nc.scalar.activation(cos_ph[:], abs_rel[:], FUNC.Sin, bias=half_pi[:], scale=-PHASE_PER_REL)
-
-        re_ent_sq = held.tile([D, S], F32, name="re_ent_sq")
-        nc.vector.tensor_tensor(re_ent_sq[:], re_ent[:], re_ent[:], ALU.mult)
-        im_ent_sq = held.tile([D, S], F32, name="im_ent_sq")
-        nc.vector.tensor_tensor(im_ent_sq[:], im_ent[:], im_ent[:], ALU.mult)
-        ent_norm = held.tile([D, S], F32, name="ent_norm")
-        nc.vector.tensor_tensor(ent_norm[:], re_ent_sq[:], im_ent_sq[:], ALU.add)
-        nc.vector.tensor_scalar(ent_norm[:], ent_norm[:], GUARD, None, ALU.mult)
 
         re_cos = held.tile([D, N], F32, name="re_cos")
         nc.vector.tensor_tensor(re_cos[:], re_ent[:].indirect(offsets[:]), cos_ph[:], ALU.mult)
@@ -64,52 +75,65 @@ def tile_rotate_kernel(tc, ent, rel, offs, out):
         nc.vector.tensor_tensor(re_sin[:], re_ent[:].indirect(offsets[:]), sin_ph[:], ALU.mult)
         im_cos = held.tile([D, N], F32, name="im_cos")
         nc.vector.tensor_tensor(im_cos[:], im_ent[:].indirect(offsets[:]), cos_ph[:], ALU.mult)
-        re_rot = held.tile([D, N], F32, name="re_rot")
-        nc.vector.tensor_tensor(re_rot[:], re_cos[:], im_sin[:], ALU.subtract)
-        im_rot = held.tile([D, N], F32, name="im_rot")
-        nc.vector.tensor_tensor(im_rot[:], re_sin[:], im_cos[:], ALU.add)
+        rot = held.tile([D, 2 * N], F32, name="rot")
+        nc.vector.tensor_tensor(rot[:, 0:N], re_cos[:], im_sin[:], ALU.subtract)
+        nc.vector.tensor_tensor(rot[:, N : 2 * N], re_sin[:], im_cos[:], ALU.add)
 
-        re_coef = held.tile([D, N], F32, name="re_coef")
-        nc.vector.tensor_scalar(re_coef[:], re_rot[:], -2.0, None, ALU.mult)
-        im_coef = held.tile([D, N], F32, name="im_coef")
-        nc.vector.tensor_scalar(im_coef[:], im_rot[:], -2.0, None, ALU.mult)
-        re_rot_sq = held.tile([D, N], F32, name="re_rot_sq")
-        nc.vector.tensor_tensor(re_rot_sq[:], re_rot[:], re_rot[:], ALU.mult)
-        im_rot_sq = held.tile([D, N], F32, name="im_rot_sq")
-        nc.vector.tensor_tensor(im_rot_sq[:], im_rot[:], im_rot[:], ALU.mult)
-        rot_norm = held.tile([D, N], F32, name="rot_norm")
-        nc.vector.tensor_tensor(rot_norm[:], re_rot_sq[:], im_rot_sq[:], ALU.add)
-        nc.vector.tensor_scalar(rot_norm[:], rot_norm[:], GUARD, None, ALU.mult)
+        query = held.tile([D, 3 * N], F32, name="query")
+        nc.vector.tensor_scalar(query[:, 0 : 2 * N], rot[:], -2.0, None, ALU.mult)
+        rot_sq = held.tile([D, 2 * N], F32, name="rot_sq")
+        nc.vector.tensor_tensor(rot_sq[:], rot[:], rot[:], ALU.mult)
+        nc.vector.tensor_tensor(query[:, 2 * N : 3 * N], rot_sq[:, 0:N], rot_sq[:, N : 2 * N], ALU.add)
+        nc.vector.tensor_scalar(query[:, 2 * N : 3 * N], query[:, 2 * N : 3 * N], GUARD, None, ALU.mult)
+        query_pieces = split(query[:], "query", nc.vector.tensor_copy)
+        re_coef = [piece[:, 0:N] for piece in query_pieces]
+        im_coef = [piece[:, N : 2 * N] for piece in query_pieces]
+        rot_norm = [piece[:, 2 * N : 3 * N] for piece in query_pieces]
 
-        dist_sum = psum.tile([N, S], F32, name="dist_sum")
-        for j in range(N):
-            modulus = work.tile([D, S], BF16, name="modulus")
-            if j % 3 == 0:
-                re_sq = work.tile([D, S], F32, name="re_sq")
-                nc.scalar.activation(re_sq[:], re_ent[:], FUNC.Square, bias=re_rot[:, j : j + 1], scale=-1.0)
-                im_sq = work.tile([D, S], F32, name="im_sq")
-                nc.scalar.activation(im_sq[:], im_ent[:], FUNC.Square, bias=im_rot[:, j : j + 1], scale=-1.0)
-                mod_sq = work.tile([D, S], F32, name="mod_sq")
-                nc.vector.tensor_tensor(mod_sq[:], re_sq[:], im_sq[:], ALU.add)
-                nc.scalar.activation(modulus[:], mod_sq[:], FUNC.Sqrt)
-            else:
-                partial = work.tile([D, S], F32, name="partial")
-                nc.vector.scalar_tensor_tensor(
-                    partial[:], re_ent[:], re_coef[:, j : j + 1], ent_norm[:], ALU.mult, ALU.add
-                )
-                cross = work.tile([D, S], F32, name="cross")
-                nc.vector.scalar_tensor_tensor(
-                    cross[:], im_ent[:], im_coef[:, j : j + 1], partial[:], ALU.mult, ALU.add
-                )
-                nc.scalar.activation(modulus[:], cross[:], FUNC.Sqrt, bias=rot_norm[:, j : j + 1])
+        re_basis = [piece[:] for piece in split(re_ent[:], "re_ent", nc.scalar.copy)]
+        im_basis = [piece[:] for piece in split(im_ent[:], "im_ent", nc.scalar.copy)]
+        re_ent_sq = held.tile([D, S], F32, name="re_ent_sq")
+        nc.scalar.activation(re_ent_sq[:], re_ent[:], FUNC.Square)
+        im_ent_sq = held.tile([D, S], F32, name="im_ent_sq")
+        nc.scalar.activation(im_ent_sq[:], im_ent[:], FUNC.Square)
+        ent_norm = held.tile([D, S], F32, name="ent_norm")
+        nc.vector.tensor_tensor(ent_norm[:], re_ent_sq[:], im_ent_sq[:], ALU.add)
+        nc.vector.tensor_scalar(ent_norm[:], ent_norm[:], GUARD, None, ALU.mult)
+        norm_basis = [piece[:] for piece in split(ent_norm[:], "ent_norm", nc.scalar.copy)]
+
+        factors = []
+        for i, (a, b) in enumerate(PAIRS):
+            factors.append((re_coef[a], re_basis[b]))
+            factors.append((im_coef[a], im_basis[b]))
+            if i < 3:
+                factors.append((rot_norm[i], ones[:]))
+                factors.append((ones[:, 0:N], norm_basis[i]))
+        coef_rows = held.tile([K, D * N], BF16, name="coef_rows")
+        basis_rows = held.tile([K, D * S], BF16, name="basis_rows")
+        port_by_port = sorted(range(K), key=lambda r: r % 4)
+
+        for d0, d1 in BLOCKS:
+            for r in port_by_port:
+                coef, basis = factors[r]
+                nc.sync.dma_start(basis_rows[r : r + 1, d0 * S : d1 * S], basis[d0:d1, :])
+                nc.sync.dma_start(coef_rows[r : r + 1, d0 * N : d1 * N], coef[d0:d1, :])
+
+        for d in range(D):
+            mod_sq = banks.tile([N, S], F32, name="mod_sq")
             nc.tensor.matmul(
-                dist_sum[:],
-                pick_row[:, N - 1 - j : 2 * N - 1 - j],
-                modulus[:],
-                start=(j == 0),
-                stop=(j == N - 1),
+                mod_sq[:],
+                coef_rows[:, d * N : (d + 1) * N],
+                basis_rows[:, d * S : (d + 1) * S],
+                start=True,
+                stop=True,
             )
+            modulus = work.tile([N, S], F32, name="modulus")
+            nc.scalar.activation(modulus[:], mod_sq[:], FUNC.Sqrt)
+            dist_sum = dist_sums[d % 2]
+            nc.vector.tensor_tensor(dist_sum[:], dist_sum[:], modulus[:], ALU.add)
 
         score = held.tile([N, S], F32, name="score")
-        nc.vector.tensor_scalar(score[:], dist_sum[:], -1.0, GAMMA, ALU.mult, ALU.add)
+        nc.vector.scalar_tensor_tensor(
+            score[:], dist_sums[0][:], -1.0, dist_sums[1][:], ALU.mult, ALU.subtract
+        )
         nc.sync.dma_start(out, score[:])

@@ -1,6 +1,7 @@
 import math
 
 import concourse.mybir as mybir
+from concourse.masks import make_identity
 
 F32 = mybir.dt.float32
 BF16 = mybir.dt.bfloat16
@@ -15,9 +16,9 @@ GAMMA = 12.0
 PHASE_PER_REL = math.pi / 0.028
 
 PAIRS = [(a, b) for a in range(3) for b in range(3 - a)]
-K = 2 * len(PAIRS) + 3 + 3
+K = 2 * len(PAIRS) + 3
 
-BLOCKS = ((0, 16), (16, 32), (32, 64), (64, D))
+BLOCK = 32
 
 GUARD = 1.0 + 2.0**-18
 
@@ -30,6 +31,7 @@ def tile_rotate_kernel(tc, ent, rel, offs, out):
         tc.tile_pool(name="held", bufs=1) as held,
         tc.tile_pool(name="work", bufs=3) as work,
         tc.psum_pool(name="banks", bufs=4) as banks,
+        tc.psum_pool(name="once", bufs=1) as once,
     ):
         offsets = held.tile([128, N // 16], U16, name="offsets")
         nc.sync.dma_start(offsets[:], offs)
@@ -40,8 +42,10 @@ def tile_rotate_kernel(tc, ent, rel, offs, out):
         im_ent = held.tile([D, S], F32, name="im_ent")
         nc.scalar.dma_start(im_ent[:], ent[D : 2 * D, :])
 
-        ones = held.tile([D, S], BF16, name="ones")
+        ones = held.tile([D, N], BF16, name="ones")
         nc.gpsimd.memset(ones[:], 1.0)
+        identity = held.tile([D, D], F32, name="identity")
+        make_identity(nc, identity[:])
         dist_sums = [held.tile([N, S], F32, name=f"dist_sum{i}") for i in range(2)]
         nc.gpsimd.memset(dist_sums[0][:], -GAMMA)
         nc.gpsimd.memset(dist_sums[1][:], 0.0)
@@ -79,16 +83,21 @@ def tile_rotate_kernel(tc, ent, rel, offs, out):
         nc.vector.tensor_tensor(rot[:, 0:N], re_cos[:], im_sin[:], ALU.subtract)
         nc.vector.tensor_tensor(rot[:, N : 2 * N], re_sin[:], im_cos[:], ALU.add)
 
-        query = held.tile([D, 3 * N], F32, name="query")
-        nc.vector.tensor_scalar(query[:, 0 : 2 * N], rot[:], -2.0, None, ALU.mult)
-        rot_sq = held.tile([D, 2 * N], F32, name="rot_sq")
-        nc.vector.tensor_tensor(rot_sq[:], rot[:], rot[:], ALU.mult)
-        nc.vector.tensor_tensor(query[:, 2 * N : 3 * N], rot_sq[:, 0:N], rot_sq[:, N : 2 * N], ALU.add)
-        nc.vector.tensor_scalar(query[:, 2 * N : 3 * N], query[:, 2 * N : 3 * N], GUARD, None, ALU.mult)
+        query = held.tile([D, 2 * N], F32, name="query")
+        nc.vector.tensor_scalar(query[:], rot[:], -2.0, None, ALU.mult)
         query_pieces = split(query[:], "query", nc.vector.tensor_copy)
         re_coef = [piece[:, 0:N] for piece in query_pieces]
         im_coef = [piece[:, N : 2 * N] for piece in query_pieces]
-        rot_norm = [piece[:, 2 * N : 3 * N] for piece in query_pieces]
+
+        rot_sq = held.tile([D, 2 * N], F32, name="rot_sq")
+        nc.vector.tensor_tensor(rot_sq[:], rot[:], rot[:], ALU.mult)
+        rot_norm = held.tile([D, N], F32, name="rot_norm")
+        nc.vector.tensor_tensor(rot_norm[:], rot_sq[:, 0:N], rot_sq[:, N : 2 * N], ALU.add)
+        nc.vector.tensor_scalar(rot_norm[:], rot_norm[:], GUARD, None, ALU.mult)
+        rot_norm_ps = once.tile([N, D], F32, name="rot_norm_ps")
+        nc.tensor.transpose(rot_norm_ps[:], rot_norm[:], identity[:])
+        rot_norm_t = held.tile([N, D], F32, name="rot_norm_t")
+        nc.vector.tensor_copy(rot_norm_t[:], rot_norm_ps[:])
 
         re_basis = [piece[:] for piece in split(re_ent[:], "re_ent", nc.scalar.copy)]
         im_basis = [piece[:] for piece in split(im_ent[:], "im_ent", nc.scalar.copy)]
@@ -102,21 +111,21 @@ def tile_rotate_kernel(tc, ent, rel, offs, out):
         norm_basis = [piece[:] for piece in split(ent_norm[:], "ent_norm", nc.scalar.copy)]
 
         factors = []
-        for i, (a, b) in enumerate(PAIRS):
+        for a, b in PAIRS:
             factors.append((re_coef[a], re_basis[b]))
             factors.append((im_coef[a], im_basis[b]))
-            if i < 3:
-                factors.append((rot_norm[i], ones[:]))
-                factors.append((ones[:, 0:N], norm_basis[i]))
+        for b in range(3):
+            factors.append((ones[:], norm_basis[b]))
         coef_rows = held.tile([K, D * N], BF16, name="coef_rows")
         basis_rows = held.tile([K, D * S], BF16, name="basis_rows")
         port_by_port = sorted(range(K), key=lambda r: r % 4)
 
-        for d0, d1 in BLOCKS:
+        for d0 in range(0, D, BLOCK):
+            d1 = d0 + BLOCK
             for r in port_by_port:
-                coef, basis = factors[r]
-                nc.sync.dma_start(basis_rows[r : r + 1, d0 * S : d1 * S], basis[d0:d1, :])
-                nc.sync.dma_start(coef_rows[r : r + 1, d0 * N : d1 * N], coef[d0:d1, :])
+                nc.sync.dma_start(basis_rows[r : r + 1, d0 * S : d1 * S], factors[r][1][d0:d1, :])
+            for r in port_by_port:
+                nc.sync.dma_start(coef_rows[r : r + 1, d0 * N : d1 * N], factors[r][0][d0:d1, :])
 
         for d in range(D):
             mod_sq = banks.tile([N, S], F32, name="mod_sq")
@@ -128,7 +137,7 @@ def tile_rotate_kernel(tc, ent, rel, offs, out):
                 stop=True,
             )
             modulus = work.tile([N, S], F32, name="modulus")
-            nc.scalar.activation(modulus[:], mod_sq[:], FUNC.Sqrt)
+            nc.scalar.activation(modulus[:], mod_sq[:], FUNC.Sqrt, bias=rot_norm_t[:, d : d + 1])
             dist_sum = dist_sums[d % 2]
             nc.vector.tensor_tensor(dist_sum[:], dist_sum[:], modulus[:], ALU.add)
 

@@ -20,7 +20,7 @@ K = 2 * len(PAIRS) + 3
 
 BLOCK = 32
 
-GUARD = 1.0 + 2.0**-18
+GUARD_ROOT = 1.0 + 2.0**-19
 
 FLOPS = 7 * D * N * S
 
@@ -90,42 +90,42 @@ def tile_rotate_kernel(tc, ent, rel, offs, out):
         im_coef = [piece[:, N : 2 * N] for piece in query_pieces]
 
         rot_sq = held.tile([D, 2 * N], F32, name="rot_sq")
-        nc.vector.tensor_tensor(rot_sq[:], rot[:], rot[:], ALU.mult)
+        nc.scalar.activation(rot_sq[:], rot[:], FUNC.Square, scale=GUARD_ROOT)
         rot_norm = held.tile([D, N], F32, name="rot_norm")
         nc.vector.tensor_tensor(rot_norm[:], rot_sq[:, 0:N], rot_sq[:, N : 2 * N], ALU.add)
-        nc.vector.tensor_scalar(rot_norm[:], rot_norm[:], GUARD, None, ALU.mult)
         rot_norm_ps = once.tile([N, D], F32, name="rot_norm_ps")
         nc.tensor.transpose(rot_norm_ps[:], rot_norm[:], identity[:])
         rot_norm_t = held.tile([N, D], F32, name="rot_norm_t")
-        nc.vector.tensor_copy(rot_norm_t[:], rot_norm_ps[:])
+        nc.scalar.copy(rot_norm_t[:], rot_norm_ps[:])
 
-        re_basis = [piece[:] for piece in split(re_ent[:], "re_ent", nc.scalar.copy)]
-        im_basis = [piece[:] for piece in split(im_ent[:], "im_ent", nc.scalar.copy)]
         re_ent_sq = held.tile([D, S], F32, name="re_ent_sq")
-        nc.scalar.activation(re_ent_sq[:], re_ent[:], FUNC.Square)
+        nc.scalar.activation(re_ent_sq[:], re_ent[:], FUNC.Square, scale=GUARD_ROOT)
         im_ent_sq = held.tile([D, S], F32, name="im_ent_sq")
-        nc.scalar.activation(im_ent_sq[:], im_ent[:], FUNC.Square)
+        nc.scalar.activation(im_ent_sq[:], im_ent[:], FUNC.Square, scale=GUARD_ROOT)
         ent_norm = held.tile([D, S], F32, name="ent_norm")
         nc.vector.tensor_tensor(ent_norm[:], re_ent_sq[:], im_ent_sq[:], ALU.add)
-        nc.vector.tensor_scalar(ent_norm[:], ent_norm[:], GUARD, None, ALU.mult)
         norm_basis = [piece[:] for piece in split(ent_norm[:], "ent_norm", nc.scalar.copy)]
+        re_basis = [piece[:] for piece in split(re_ent[:], "re_ent", nc.scalar.copy)]
+        im_basis = [piece[:] for piece in split(im_ent[:], "im_ent", nc.scalar.copy)]
 
-        factors = []
-        for a, b in PAIRS:
-            factors.append((re_coef[a], re_basis[b]))
-            factors.append((im_coef[a], im_basis[b]))
-        for b in range(3):
-            factors.append((ones[:], norm_basis[b]))
         coef_rows = held.tile([K, D * N], BF16, name="coef_rows")
         basis_rows = held.tile([K, D * S], BF16, name="basis_rows")
-        port_by_port = sorted(range(K), key=lambda r: r % 4)
-
+        factors = []
+        for a, b in PAIRS:
+            factors.append((4 + a, re_coef[a], 1 + b, re_basis[b]))
+            factors.append((4 + a, im_coef[a], 1 + b, im_basis[b]))
+        for b in range(3):
+            factors.append((0, ones[:], 2 + b, norm_basis[b]))
+        sends = []
+        for r, (coef_rank, coef, basis_rank, basis) in enumerate(factors):
+            sends.append((coef_rank, coef_rows[r : r + 1, :], coef))
+            sends.append((basis_rank, basis_rows[r : r + 1, :], basis))
+        sends.sort(key=lambda send: send[0])
         for d0 in range(0, D, BLOCK):
             d1 = d0 + BLOCK
-            for r in port_by_port:
-                nc.sync.dma_start(basis_rows[r : r + 1, d0 * S : d1 * S], factors[r][1][d0:d1, :])
-            for r in port_by_port:
-                nc.sync.dma_start(coef_rows[r : r + 1, d0 * N : d1 * N], factors[r][0][d0:d1, :])
+            for rank, row, array in sends:
+                width = array.shape[1]
+                nc.sync.dma_start(row[:, d0 * width : d1 * width], array[d0:d1, :])
 
         for d in range(D):
             mod_sq = banks.tile([N, S], F32, name="mod_sq")

@@ -15,12 +15,12 @@ N = 128
 GAMMA = 12.0
 PHASE_PER_REL = math.pi / 0.028
 
-PAIRS = [(a, b) for a in range(3) for b in range(3 - a)]
+PAIRS = [(a, b) for b in range(3) for a in range(3 - b)]
 K = 2 * len(PAIRS) + 3
 
 BLOCK = 32
 
-GUARD_ROOT = 1.0 + 2.0**-19
+GUARD = 1.0 + 2.0**-18
 
 FLOPS = 7 * D * N * S
 
@@ -90,42 +90,41 @@ def tile_rotate_kernel(tc, ent, rel, offs, out):
         im_coef = [piece[:, N : 2 * N] for piece in query_pieces]
 
         rot_sq = held.tile([D, 2 * N], F32, name="rot_sq")
-        nc.scalar.activation(rot_sq[:], rot[:], FUNC.Square, scale=GUARD_ROOT)
+        nc.vector.tensor_tensor(rot_sq[:], rot[:], rot[:], ALU.mult)
         rot_norm = held.tile([D, N], F32, name="rot_norm")
         nc.vector.tensor_tensor(rot_norm[:], rot_sq[:, 0:N], rot_sq[:, N : 2 * N], ALU.add)
+        nc.vector.tensor_scalar(rot_norm[:], rot_norm[:], GUARD, None, ALU.mult)
         rot_norm_ps = once.tile([N, D], F32, name="rot_norm_ps")
         nc.tensor.transpose(rot_norm_ps[:], rot_norm[:], identity[:])
         rot_norm_t = held.tile([N, D], F32, name="rot_norm_t")
-        nc.scalar.copy(rot_norm_t[:], rot_norm_ps[:])
+        nc.vector.tensor_copy(rot_norm_t[:], rot_norm_ps[:])
 
-        re_ent_sq = held.tile([D, S], F32, name="re_ent_sq")
-        nc.scalar.activation(re_ent_sq[:], re_ent[:], FUNC.Square, scale=GUARD_ROOT)
-        im_ent_sq = held.tile([D, S], F32, name="im_ent_sq")
-        nc.scalar.activation(im_ent_sq[:], im_ent[:], FUNC.Square, scale=GUARD_ROOT)
-        ent_norm = held.tile([D, S], F32, name="ent_norm")
-        nc.vector.tensor_tensor(ent_norm[:], re_ent_sq[:], im_ent_sq[:], ALU.add)
-        norm_basis = [piece[:] for piece in split(ent_norm[:], "ent_norm", nc.scalar.copy)]
         re_basis = [piece[:] for piece in split(re_ent[:], "re_ent", nc.scalar.copy)]
         im_basis = [piece[:] for piece in split(im_ent[:], "im_ent", nc.scalar.copy)]
+        re_ent_sq = held.tile([D, S], F32, name="re_ent_sq")
+        nc.scalar.activation(re_ent_sq[:], re_ent[:], FUNC.Square)
+        im_ent_sq = held.tile([D, S], F32, name="im_ent_sq")
+        nc.scalar.activation(im_ent_sq[:], im_ent[:], FUNC.Square)
+        ent_norm = held.tile([D, S], F32, name="ent_norm")
+        nc.vector.tensor_tensor(ent_norm[:], re_ent_sq[:], im_ent_sq[:], ALU.add)
+        nc.vector.tensor_scalar(ent_norm[:], ent_norm[:], GUARD, None, ALU.mult)
+        norm_basis = [piece[:] for piece in split(ent_norm[:], "ent_norm", nc.scalar.copy)]
 
-        coef_rows = held.tile([K, D * N], BF16, name="coef_rows")
-        basis_rows = held.tile([K, D * S], BF16, name="basis_rows")
         factors = []
         for a, b in PAIRS:
-            factors.append((4 + a, re_coef[a], 1 + b, re_basis[b]))
-            factors.append((4 + a, im_coef[a], 1 + b, im_basis[b]))
+            factors.append((re_coef[a], re_basis[b]))
+            factors.append((im_coef[a], im_basis[b]))
         for b in range(3):
-            factors.append((0, ones[:], 2 + b, norm_basis[b]))
-        sends = []
-        for r, (coef_rank, coef, basis_rank, basis) in enumerate(factors):
-            sends.append((coef_rank, coef_rows[r : r + 1, :], coef))
-            sends.append((basis_rank, basis_rows[r : r + 1, :], basis))
-        sends.sort(key=lambda send: send[0])
+            factors.append((ones[:], norm_basis[b]))
+        rows = [4 * (i % 4) + i // 4 for i in range(K)]
+        coef_rows = held.tile([K, D * N], BF16, name="coef_rows")
+        basis_rows = held.tile([K, D * S], BF16, name="basis_rows")
         for d0 in range(0, D, BLOCK):
             d1 = d0 + BLOCK
-            for rank, row, array in sends:
-                width = array.shape[1]
-                nc.sync.dma_start(row[:, d0 * width : d1 * width], array[d0:d1, :])
+            for r, (coef, basis) in zip(rows, factors):
+                nc.sync.dma_start(basis_rows[r : r + 1, d0 * S : d1 * S], basis[d0:d1, :])
+            for r, (coef, basis) in zip(rows, factors):
+                nc.sync.dma_start(coef_rows[r : r + 1, d0 * N : d1 * N], coef[d0:d1, :])
 
         for d in range(D):
             mod_sq = banks.tile([N, S], F32, name="mod_sq")

@@ -1,7 +1,7 @@
 import math
 
 import concourse.mybir as mybir
-from concourse.masks import make_identity
+from concourse.masks import make_block_diagonal, make_identity
 
 F32 = mybir.dt.float32
 BF16 = mybir.dt.bfloat16
@@ -16,11 +16,22 @@ GAMMA = 12.0
 PHASE_PER_REL = math.pi / 0.028
 
 PAIRS = [(a, b) for b in range(3) for a in range(3 - b)]
-K = 2 * len(PAIRS) + 3
+NORM_SLOT = 2 * len(PAIRS)
+SLOTS = 16
+GROUPS = 128 // SLOTS
+SETS = D // GROUPS
 
-BLOCK = 32
+APART = 4
+SPAN = APART * GROUPS
 
-GUARD = 1.0 + 2.0**-18
+
+def set_start(t):
+    return SPAN * (t // APART) + t % APART
+
+
+GUARD_ROOT = 1.0 + 2.0**-19
+
+AHEAD = 3
 
 FLOPS = 7 * D * N * S
 
@@ -29,8 +40,8 @@ def tile_rotate_kernel(tc, ent, rel, offs, out):
     nc = tc.nc
     with (
         tc.tile_pool(name="held", bufs=1) as held,
-        tc.tile_pool(name="work", bufs=3) as work,
-        tc.psum_pool(name="banks", bufs=4) as banks,
+        tc.tile_pool(name="work", bufs=AHEAD + 1) as work,
+        tc.psum_pool(name="banks", bufs=AHEAD + 2) as banks,
         tc.psum_pool(name="once", bufs=1) as once,
     ):
         offsets = held.tile([128, N // 16], U16, name="offsets")
@@ -42,27 +53,29 @@ def tile_rotate_kernel(tc, ent, rel, offs, out):
         im_ent = held.tile([D, S], F32, name="im_ent")
         nc.scalar.dma_start(im_ent[:], ent[D : 2 * D, :])
 
-        ones = held.tile([D, N], BF16, name="ones")
-        nc.gpsimd.memset(ones[:], 1.0)
         identity = held.tile([D, D], F32, name="identity")
         make_identity(nc, identity[:])
-        dist_sums = [held.tile([N, S], F32, name=f"dist_sum{i}") for i in range(2)]
-        nc.gpsimd.memset(dist_sums[0][:], -GAMMA)
-        nc.gpsimd.memset(dist_sums[1][:], 0.0)
+        identity_bf = held.tile([N, N], BF16, name="identity_bf")
+        make_identity(nc, identity_bf[:])
+        own_group = held.tile([128, 128], F32, name="own_group")
+        make_block_diagonal(nc, own_group[:], SLOTS)
         half_pi = held.tile([D, 1], F32, name="half_pi")
         nc.vector.memset(half_pi[:], math.pi / 2)
 
-        def split(value, name, cast):
-            shape = [D, value.shape[1]]
-            high = held.tile(shape, BF16, name=name + "_high")
-            cast(high[:], value)
-            rest = held.tile(shape, F32, name=name + "_rest")
-            nc.vector.tensor_tensor(rest[:], value, high[:], ALU.subtract)
-            middle = held.tile(shape, BF16, name=name + "_middle")
-            cast(middle[:], rest[:])
-            low = held.tile(shape, BF16, name=name + "_low")
-            nc.vector.tensor_tensor(low[:], rest[:], middle[:], ALU.subtract)
-            return high, middle, low
+        query_slots = held.tile([D, SLOTS * N], BF16, name="query_slots")
+        table_slots = held.tile([D, SLOTS * S], BF16, name="table_slots")
+        nc.gpsimd.memset(query_slots[:, NORM_SLOT * N : (NORM_SLOT + 3) * N], 1.0)
+        nc.gpsimd.memset(query_slots[:, (SLOTS - 1) * N :], 0.0)
+        nc.gpsimd.memset(table_slots[:, (SLOTS - 1) * S :], 0.0)
+
+        def split(value, rest, homes, cast, copy):
+            cast(homes[0][0], value)
+            nc.vector.tensor_tensor(rest, value, homes[0][0], ALU.subtract)
+            cast(homes[1][0], rest)
+            nc.vector.tensor_tensor(homes[2][0], rest, homes[1][0], ALU.subtract)
+            for places in homes:
+                for place in places[1:]:
+                    copy(place, places[0])
 
         sin_ph = held.tile([D, N], F32, name="sin_ph")
         nc.scalar.activation(sin_ph[:], rel_sb[:], FUNC.Sin, scale=PHASE_PER_REL)
@@ -85,63 +98,107 @@ def tile_rotate_kernel(tc, ent, rel, offs, out):
 
         query = held.tile([D, 2 * N], F32, name="query")
         nc.vector.tensor_scalar(query[:], rot[:], -2.0, None, ALU.mult)
-        query_pieces = split(query[:], "query", nc.vector.tensor_copy)
-        re_coef = [piece[:, 0:N] for piece in query_pieces]
-        im_coef = [piece[:, N : 2 * N] for piece in query_pieces]
+        query_rest = held.tile([D, 2 * N], F32, name="query_rest")
+        by_slot = query_slots[:].rearrange("p (k n) -> p k n", n=N)
+        split(
+            query[:].rearrange("p (x n) -> p x n", n=N),
+            query_rest[:].rearrange("p (x n) -> p x n", n=N),
+            [
+                [by_slot[:, i : i + len(PAIRS) + 1 : len(PAIRS), :] for i, (a, b) in enumerate(PAIRS) if a == piece]
+                for piece in range(3)
+            ],
+            nc.vector.tensor_copy,
+            nc.vector.tensor_copy,
+        )
+
+        def table_slot(k):
+            return table_slots[:, k * S : (k + 1) * S]
+
+        re_ent_sq = held.tile([D, S], F32, name="re_ent_sq")
+        nc.scalar.activation(re_ent_sq[:], re_ent[:], FUNC.Square, scale=GUARD_ROOT)
+        im_ent_sq = held.tile([D, S], F32, name="im_ent_sq")
+        nc.scalar.activation(im_ent_sq[:], im_ent[:], FUNC.Square, scale=GUARD_ROOT)
+        ent_norm = held.tile([D, S], F32, name="ent_norm")
+        nc.vector.tensor_tensor(ent_norm[:], re_ent_sq[:], im_ent_sq[:], ALU.add)
+        norm_rest = held.tile([D, S], F32, name="norm_rest")
+        split(
+            ent_norm[:],
+            norm_rest[:],
+            [[table_slot(NORM_SLOT + piece)] for piece in range(3)],
+            nc.vector.tensor_copy,
+            nc.vector.tensor_copy,
+        )
+        for x, part in enumerate((re_ent, im_ent)):
+            part_rest = held.tile([D, S], F32, name=f"part_rest{x}")
+            split(
+                part[:],
+                part_rest[:],
+                [
+                    [table_slot(x * len(PAIRS) + i) for i, (a, b) in enumerate(PAIRS) if b == piece]
+                    for piece in range(3)
+                ],
+                nc.scalar.copy,
+                nc.scalar.copy,
+            )
 
         rot_sq = held.tile([D, 2 * N], F32, name="rot_sq")
-        nc.vector.tensor_tensor(rot_sq[:], rot[:], rot[:], ALU.mult)
+        nc.scalar.activation(rot_sq[:], rot[:], FUNC.Square, scale=GUARD_ROOT)
         rot_norm = held.tile([D, N], F32, name="rot_norm")
         nc.vector.tensor_tensor(rot_norm[:], rot_sq[:, 0:N], rot_sq[:, N : 2 * N], ALU.add)
-        nc.vector.tensor_scalar(rot_norm[:], rot_norm[:], GUARD, None, ALU.mult)
         rot_norm_ps = once.tile([N, D], F32, name="rot_norm_ps")
         nc.tensor.transpose(rot_norm_ps[:], rot_norm[:], identity[:])
         rot_norm_t = held.tile([N, D], F32, name="rot_norm_t")
-        nc.vector.tensor_copy(rot_norm_t[:], rot_norm_ps[:])
+        nc.scalar.copy(rot_norm_t[:], rot_norm_ps[:])
 
-        re_basis = [piece[:] for piece in split(re_ent[:], "re_ent", nc.scalar.copy)]
-        im_basis = [piece[:] for piece in split(im_ent[:], "im_ent", nc.scalar.copy)]
-        re_ent_sq = held.tile([D, S], F32, name="re_ent_sq")
-        nc.scalar.activation(re_ent_sq[:], re_ent[:], FUNC.Square)
-        im_ent_sq = held.tile([D, S], F32, name="im_ent_sq")
-        nc.scalar.activation(im_ent_sq[:], im_ent[:], FUNC.Square)
-        ent_norm = held.tile([D, S], F32, name="ent_norm")
-        nc.vector.tensor_tensor(ent_norm[:], re_ent_sq[:], im_ent_sq[:], ALU.add)
-        nc.vector.tensor_scalar(ent_norm[:], ent_norm[:], GUARD, None, ALU.mult)
-        norm_basis = [piece[:] for piece in split(ent_norm[:], "ent_norm", nc.scalar.copy)]
-
-        factors = []
-        for a, b in PAIRS:
-            factors.append((re_coef[a], re_basis[b]))
-            factors.append((im_coef[a], im_basis[b]))
-        for b in range(3):
-            factors.append((ones[:], norm_basis[b]))
-        rows = [4 * (i % 4) + i // 4 for i in range(K)]
-        coef_rows = held.tile([K, D * N], BF16, name="coef_rows")
-        basis_rows = held.tile([K, D * S], BF16, name="basis_rows")
-        for d0 in range(0, D, BLOCK):
-            d1 = d0 + BLOCK
-            for r, (coef, basis) in zip(rows, factors):
-                nc.sync.dma_start(basis_rows[r : r + 1, d0 * S : d1 * S], basis[d0:d1, :])
-            for r, (coef, basis) in zip(rows, factors):
-                nc.sync.dma_start(coef_rows[r : r + 1, d0 * N : d1 * N], coef[d0:d1, :])
-
-        for d in range(D):
-            mod_sq = banks.tile([N, S], F32, name="mod_sq")
-            nc.tensor.matmul(
-                mod_sq[:],
-                coef_rows[:, d * N : (d + 1) * N],
-                basis_rows[:, d * S : (d + 1) * S],
-                start=True,
-                stop=True,
+        query_rows = held.tile([128, SETS * N], BF16, name="query_rows")
+        table_rows = held.tile([128, SETS * S], BF16, name="table_rows")
+        for rows, slots, width in ((query_rows, query_slots, N), (table_rows, table_slots, S)):
+            for t in range(SETS):
+                last = set_start(t) + APART * (GROUPS - 1)
+                nc.sync.dma_start(
+                    rows[:, t * width : (t + 1) * width], slots[set_start(t) : last + 1 : APART, :]
+                )
+        weights = held.tile([128, D * N], BF16, name="weights")
+        for d in range(0, D, APART):
+            t = APART * (d // SPAN)
+            g = d % SPAN // APART
+            nc.vector.tensor_scalar(
+                weights[:, d * N : (d + APART) * N],
+                query_rows[:, t * N : (t + APART) * N],
+                own_group[:, SLOTS * g : SLOTS * g + 1],
+                None,
+                ALU.mult,
             )
-            modulus = work.tile([N, S], F32, name="modulus")
-            nc.scalar.activation(modulus[:], mod_sq[:], FUNC.Sqrt, bias=rot_norm_t[:, d : d + 1])
-            dist_sum = dist_sums[d % 2]
-            nc.vector.tensor_tensor(dist_sum[:], dist_sum[:], modulus[:], ALU.add)
+
+        order = [(t, set_start(t) + APART * g) for t in range(SETS) for g in range(GROUPS)]
+        dist_sum = once.tile([N, S], F32, name="dist_sum")
+        products = []
+        for step in range(D + AHEAD):
+            if step < D:
+                t, d = order[step]
+                mod_sq = banks.tile([N, S], F32, name="mod_sq")
+                nc.tensor.matmul(
+                    mod_sq[:],
+                    weights[:, d * N : (d + 1) * N],
+                    table_rows[:, t * S : (t + 1) * S],
+                    start=True,
+                    stop=True,
+                )
+                products.append(mod_sq)
+            if step >= AHEAD:
+                t, d = order[step - AHEAD]
+                modulus = work.tile([N, S], BF16, name="modulus")
+                nc.scalar.activation(
+                    modulus[:], products[step - AHEAD][:], FUNC.Sqrt, bias=rot_norm_t[:, d : d + 1]
+                )
+                nc.tensor.matmul(
+                    dist_sum[:],
+                    identity_bf[:],
+                    modulus[:],
+                    start=(step == AHEAD),
+                    stop=(step == D + AHEAD - 1),
+                )
 
         score = held.tile([N, S], F32, name="score")
-        nc.vector.scalar_tensor_tensor(
-            score[:], dist_sums[0][:], -1.0, dist_sums[1][:], ALU.mult, ALU.subtract
-        )
+        nc.vector.tensor_scalar(score[:], dist_sum[:], -1.0, GAMMA, ALU.mult, ALU.add)
         nc.sync.dma_start(out, score[:])

@@ -15,14 +15,17 @@ N = 128
 GAMMA = 12.0
 PHASE_PER_REL = math.pi / 0.028
 
-PAIRS = [(a, b) for b in range(3) for a in range(3 - b)]
-NORM_SLOT = 2 * len(PAIRS)
+REPEATS = [(1, 0), (2, 0), (1, 1)]
+REPEAT_SLOT = 9
 SLOTS = 16
 GROUPS = 128 // SLOTS
 SETS = D // GROUPS
 
 APART = 4
 SPAN = APART * GROUPS
+
+PARTS = 128 // SPAN
+CHUNK = S // PARTS
 
 
 def set_start(t):
@@ -32,6 +35,7 @@ def set_start(t):
 GUARD_ROOT = 1.0 + 2.0**-19
 
 AHEAD = 3
+LAST = 2
 
 FLOPS = 7 * D * N * S
 
@@ -44,105 +48,128 @@ def tile_rotate_kernel(tc, ent, rel, offs, out):
         tc.psum_pool(name="banks", bufs=AHEAD + 2) as banks,
         tc.psum_pool(name="once", bufs=1) as once,
     ):
-        offsets = held.tile([128, N // 16], U16, name="offsets")
-        nc.sync.dma_start(offsets[:], offs)
+        early_values = held.tile([128, 3 * CHUNK], F32, name="early_values")
+        for x in range(2):
+            nc.sync.dma_start(
+                early_values[:, x * CHUNK : (x + 1) * CHUNK],
+                ent[x * D : x * D + SPAN, :].rearrange("d (c y) -> (d c) y", y=CHUNK),
+            )
         rel_sb = held.tile([D, N], F32, name="rel_sb")
         nc.scalar.dma_start(rel_sb[:], rel)
+        offsets = held.tile([128, N // 16], U16, name="offsets")
+        nc.sync.dma_start(offsets[:], offs)
         re_ent = held.tile([D, S], F32, name="re_ent")
         nc.sync.dma_start(re_ent[:], ent[0:D, :])
         im_ent = held.tile([D, S], F32, name="im_ent")
         nc.scalar.dma_start(im_ent[:], ent[D : 2 * D, :])
 
-        identity = held.tile([D, D], F32, name="identity")
-        make_identity(nc, identity[:])
-        identity_bf = held.tile([N, N], BF16, name="identity_bf")
-        make_identity(nc, identity_bf[:])
-        own_group = held.tile([128, 128], F32, name="own_group")
-        make_block_diagonal(nc, own_group[:], SLOTS)
         half_pi = held.tile([D, 1], F32, name="half_pi")
         nc.vector.memset(half_pi[:], math.pi / 2)
-
         query_slots = held.tile([D, SLOTS * N], BF16, name="query_slots")
+        early_slots = held.tile([128, SLOTS * CHUNK], BF16, name="early_slots")
         table_slots = held.tile([D, SLOTS * S], BF16, name="table_slots")
-        nc.gpsimd.memset(query_slots[:, NORM_SLOT * N : (NORM_SLOT + 3) * N], 1.0)
+        for b in range(3):
+            nc.gpsimd.memset(query_slots[:, (3 * b + 2) * N : (3 * b + 3) * N], 1.0)
         nc.gpsimd.memset(query_slots[:, (SLOTS - 1) * N :], 0.0)
+        nc.gpsimd.memset(early_slots[:, (SLOTS - 1) * CHUNK :], 0.0)
         nc.gpsimd.memset(table_slots[:, (SLOTS - 1) * S :], 0.0)
+        identity = held.tile([D, D], F32, name="identity")
+        make_identity(nc, identity[:])
+        own_group = held.tile([128, 128], F32, name="own_group")
+        make_block_diagonal(nc, own_group[:], SLOTS)
+        identity_bf = held.tile([N, N], BF16, name="identity_bf")
+        make_identity(nc, identity_bf[:])
+        table_values = held.tile([D, 3 * S], F32, name="table_values")
+        for x in range(2):
+            nc.gpsimd.dma_start(table_values[:, x * S : (x + 1) * S], ent[x * D : (x + 1) * D, :])
 
-        def split(value, rest, homes, cast, copy):
-            cast(homes[0][0], value)
-            nc.vector.tensor_tensor(rest, value, homes[0][0], ALU.subtract)
-            cast(homes[1][0], rest)
-            nc.vector.tensor_tensor(homes[2][0], rest, homes[1][0], ALU.subtract)
-            for places in homes:
-                for place in places[1:]:
-                    copy(place, places[0])
+        def enlarged_squares(re_part, im_part, width, name):
+            squares = held.tile([128, 2 * width], F32, name=name)
+            for x, part in enumerate((re_part, im_part)):
+                nc.scalar.activation(
+                    squares[:, x * width : (x + 1) * width], part, FUNC.Square, scale=GUARD_ROOT
+                )
+            return squares
 
-        sin_ph = held.tile([D, N], F32, name="sin_ph")
-        nc.scalar.activation(sin_ph[:], rel_sb[:], FUNC.Sin, scale=PHASE_PER_REL)
-        abs_rel = held.tile([D, N], F32, name="abs_rel")
-        nc.scalar.activation(abs_rel[:], rel_sb[:], FUNC.Abs)
-        cos_ph = held.tile([D, N], F32, name="cos_ph")
-        nc.scalar.activation(cos_ph[:], abs_rel[:], FUNC.Sin, bias=half_pi[:], scale=-PHASE_PER_REL)
-
-        re_cos = held.tile([D, N], F32, name="re_cos")
-        nc.vector.tensor_tensor(re_cos[:], re_ent[:].indirect(offsets[:]), cos_ph[:], ALU.mult)
-        im_sin = held.tile([D, N], F32, name="im_sin")
-        nc.vector.tensor_tensor(im_sin[:], im_ent[:].indirect(offsets[:]), sin_ph[:], ALU.mult)
-        re_sin = held.tile([D, N], F32, name="re_sin")
-        nc.vector.tensor_tensor(re_sin[:], re_ent[:].indirect(offsets[:]), sin_ph[:], ALU.mult)
-        im_cos = held.tile([D, N], F32, name="im_cos")
-        nc.vector.tensor_tensor(im_cos[:], im_ent[:].indirect(offsets[:]), cos_ph[:], ALU.mult)
-        rot = held.tile([D, 2 * N], F32, name="rot")
-        nc.vector.tensor_tensor(rot[:, 0:N], re_cos[:], im_sin[:], ALU.subtract)
-        nc.vector.tensor_tensor(rot[:, N : 2 * N], re_sin[:], im_cos[:], ALU.add)
-
-        query = held.tile([D, 2 * N], F32, name="query")
-        nc.vector.tensor_scalar(query[:], rot[:], -2.0, None, ALU.mult)
-        query_rest = held.tile([D, 2 * N], F32, name="query_rest")
-        by_slot = query_slots[:].rearrange("p (k n) -> p k n", n=N)
-        split(
-            query[:].rearrange("p (x n) -> p x n", n=N),
-            query_rest[:].rearrange("p (x n) -> p x n", n=N),
-            [
-                [by_slot[:, i : i + len(PAIRS) + 1 : len(PAIRS), :] for i, (a, b) in enumerate(PAIRS) if a == piece]
-                for piece in range(3)
-            ],
-            nc.vector.tensor_copy,
-            nc.vector.tensor_copy,
-        )
-
-        def table_slot(k):
-            return table_slots[:, k * S : (k + 1) * S]
-
-        re_ent_sq = held.tile([D, S], F32, name="re_ent_sq")
-        nc.scalar.activation(re_ent_sq[:], re_ent[:], FUNC.Square, scale=GUARD_ROOT)
-        im_ent_sq = held.tile([D, S], F32, name="im_ent_sq")
-        nc.scalar.activation(im_ent_sq[:], im_ent[:], FUNC.Square, scale=GUARD_ROOT)
-        ent_norm = held.tile([D, S], F32, name="ent_norm")
-        nc.vector.tensor_tensor(ent_norm[:], re_ent_sq[:], im_ent_sq[:], ALU.add)
-        norm_rest = held.tile([D, S], F32, name="norm_rest")
-        split(
-            ent_norm[:],
-            norm_rest[:],
-            [[table_slot(NORM_SLOT + piece)] for piece in range(3)],
-            nc.vector.tensor_copy,
-            nc.vector.tensor_copy,
-        )
-        for x, part in enumerate((re_ent, im_ent)):
-            part_rest = held.tile([D, S], F32, name=f"part_rest{x}")
-            split(
-                part[:],
-                part_rest[:],
-                [
-                    [table_slot(x * len(PAIRS) + i) for i, (a, b) in enumerate(PAIRS) if b == piece]
-                    for piece in range(3)
-                ],
-                nc.scalar.copy,
-                nc.scalar.copy,
+        def add_squares(values, squares, width):
+            nc.vector.tensor_tensor(
+                values[:, 2 * width :], squares[:, 0:width], squares[:, width:], ALU.add
             )
 
+        def piece(slots, width, b):
+            return slots[:, 3 * b * width : 3 * (b + 1) * width]
+
+        def pair(slots, width, k):
+            return slots[:, k * width : (k + 2) * width]
+
+        def high_and_middle(values, rest, slots, width):
+            nc.vector.tensor_copy(piece(slots, width, 0), values[:])
+            nc.vector.tensor_tensor(rest[:], values[:], piece(slots, width, 0), ALU.subtract)
+            nc.vector.tensor_copy(piece(slots, width, 1), rest[:])
+
+        def low(rest, slots, width):
+            nc.vector.tensor_tensor(
+                piece(slots, width, 2), rest[:], piece(slots, width, 1), ALU.subtract
+            )
+
+        def repeats(slots, width, copy):
+            for i, (a, b) in enumerate(REPEATS):
+                copy(pair(slots, width, REPEAT_SLOT + 2 * i), pair(slots, width, 3 * b))
+
+        early_sq = enlarged_squares(
+            early_values[:, 0:CHUNK], early_values[:, CHUNK : 2 * CHUNK], CHUNK, "early_sq"
+        )
+        add_squares(early_values, early_sq, CHUNK)
+        early_rest = held.tile([128, 3 * CHUNK], F32, name="early_rest")
+        high_and_middle(early_values, early_rest, early_slots, CHUNK)
+        low(early_rest, early_slots, CHUNK)
+        trig = held.tile([D, 2 * N], F32, name="trig")
+        nc.scalar.activation(trig[:, N : 2 * N], rel_sb[:], FUNC.Sin, scale=PHASE_PER_REL)
+        abs_rel = held.tile([D, N], F32, name="abs_rel")
+        nc.scalar.activation(abs_rel[:], rel_sb[:], FUNC.Abs)
+        nc.scalar.activation(
+            trig[:, 0:N], abs_rel[:], FUNC.Sin, bias=half_pi[:], scale=-PHASE_PER_REL
+        )
+        twice = held.tile([D, 2 * N], F32, name="twice")
+        nc.scalar.mul(twice[:], trig[:], -2.0)
+        cos2 = twice[:, 0:N]
+        sin2 = twice[:, N : 2 * N]
+        repeats(early_slots, CHUNK, nc.scalar.copy)
+        table_sq = enlarged_squares(re_ent[:], im_ent[:], S, "table_sq")
+
+        re_cos = held.tile([D, N], F32, name="re_cos")
+        nc.vector.tensor_tensor(re_cos[:], re_ent[:].indirect(offsets[:]), cos2, ALU.mult)
+        im_sin = held.tile([D, N], F32, name="im_sin")
+        nc.vector.tensor_tensor(im_sin[:], im_ent[:].indirect(offsets[:]), sin2, ALU.mult)
+        re_sin = held.tile([D, N], F32, name="re_sin")
+        nc.vector.tensor_tensor(re_sin[:], re_ent[:].indirect(offsets[:]), sin2, ALU.mult)
+        im_cos = held.tile([D, N], F32, name="im_cos")
+        nc.vector.tensor_tensor(im_cos[:], im_ent[:].indirect(offsets[:]), cos2, ALU.mult)
+        query = held.tile([D, 2 * N], F32, name="query")
+        nc.vector.tensor_tensor(query[:, 0:N], re_cos[:], im_sin[:], ALU.subtract)
+        nc.vector.tensor_tensor(query[:, N : 2 * N], re_sin[:], im_cos[:], ALU.add)
+
+        homes = [[3 * b for b in range(3)], [], []]
+        for i, (a, b) in enumerate(REPEATS):
+            homes[a].append(REPEAT_SLOT + 2 * i)
+        query_rest = held.tile([D, 2 * N], F32, name="query_rest")
+        nc.vector.tensor_copy(pair(query_slots, N, homes[0][0]), query[:])
+        nc.vector.tensor_tensor(
+            query_rest[:], query[:], pair(query_slots, N, homes[0][0]), ALU.subtract
+        )
+        nc.vector.tensor_copy(pair(query_slots, N, homes[1][0]), query_rest[:])
+        nc.vector.tensor_tensor(
+            pair(query_slots, N, homes[2][0]),
+            query_rest[:],
+            pair(query_slots, N, homes[1][0]),
+            ALU.subtract,
+        )
+
         rot_sq = held.tile([D, 2 * N], F32, name="rot_sq")
-        nc.scalar.activation(rot_sq[:], rot[:], FUNC.Square, scale=GUARD_ROOT)
+        nc.scalar.activation(rot_sq[:], query[:], FUNC.Square, scale=GUARD_ROOT / 2)
+        for slots_of_piece in homes:
+            for k in slots_of_piece[1:]:
+                nc.scalar.copy(pair(query_slots, N, k), pair(query_slots, N, slots_of_piece[0]))
         rot_norm = held.tile([D, N], F32, name="rot_norm")
         nc.vector.tensor_tensor(rot_norm[:], rot_sq[:, 0:N], rot_sq[:, N : 2 * N], ALU.add)
         rot_norm_ps = once.tile([N, D], F32, name="rot_norm_ps")
@@ -152,28 +179,59 @@ def tile_rotate_kernel(tc, ent, rel, offs, out):
 
         query_rows = held.tile([128, SETS * N], BF16, name="query_rows")
         table_rows = held.tile([128, SETS * S], BF16, name="table_rows")
-        for rows, slots, width in ((query_rows, query_slots, N), (table_rows, table_slots, S)):
-            for t in range(SETS):
-                last = set_start(t) + APART * (GROUPS - 1)
-                nc.sync.dma_start(
-                    rows[:, t * width : (t + 1) * width], slots[set_start(t) : last + 1 : APART, :]
-                )
-        weights = held.tile([128, D * N], BF16, name="weights")
-        for d in range(0, D, APART):
-            t = APART * (d // SPAN)
-            g = d % SPAN // APART
-            nc.vector.tensor_scalar(
-                weights[:, d * N : (d + APART) * N],
-                query_rows[:, t * N : (t + APART) * N],
-                own_group[:, SLOTS * g : SLOTS * g + 1],
-                None,
-                ALU.mult,
+
+        def collect(rows, slots, width, t):
+            last = set_start(t) + APART * (GROUPS - 1)
+            nc.sync.dma_start(
+                rows[:, t * width : (t + 1) * width], slots[set_start(t) : last + 1 : APART, :]
             )
+
+        def collect_early(t):
+            for c in range(PARTS):
+                first = PARTS * set_start(t) + c
+                last = first + PARTS * APART * (GROUPS - 1)
+                nc.sync.dma_start(
+                    table_rows[:, t * S + c * CHUNK : t * S + (c + 1) * CHUNK],
+                    early_slots[first : last + 1 : PARTS * APART, :],
+                )
+
+        collect_early(0)
+        for t in range(APART):
+            collect(query_rows, query_slots, N, t)
+        for t in range(1, APART):
+            collect_early(t)
+
+        weights = held.tile([128, D * N], BF16, name="weights")
+
+        def make_weights(t, count):
+            for g in range(GROUPS):
+                d = set_start(t) + APART * g
+                nc.vector.tensor_scalar(
+                    weights[:, d * N : (d + count) * N],
+                    query_rows[:, t * N : (t + count) * N],
+                    own_group[:, SLOTS * g : SLOTS * g + 1],
+                    None,
+                    ALU.mult,
+                )
+
+        make_weights(0, 1)
+        make_weights(1, APART - 1)
+        add_squares(table_values, table_sq, S)
+        table_rest = held.tile([D, 3 * S], F32, name="table_rest")
+        high_and_middle(table_values, table_rest, table_slots, S)
+        low(table_rest, table_slots, S)
+        repeats(table_slots, S, nc.vector.tensor_copy)
+        for first in range(APART, SETS, APART):
+            for t in range(first, first + APART):
+                collect(query_rows, query_slots, N, t)
+            for t in range(first, first + APART):
+                collect(table_rows, table_slots, S, t)
+            make_weights(first, APART)
 
         order = [(t, set_start(t) + APART * g) for t in range(SETS) for g in range(GROUPS)]
         dist_sum = once.tile([N, S], F32, name="dist_sum")
         products = []
-        for step in range(D + AHEAD):
+        for step in range(D + AHEAD - LAST):
             if step < D:
                 t, d = order[step]
                 mod_sq = banks.tile([N, S], F32, name="mod_sq")
@@ -196,9 +254,34 @@ def tile_rotate_kernel(tc, ent, rel, offs, out):
                     identity_bf[:],
                     modulus[:],
                     start=(step == AHEAD),
-                    stop=(step == D + AHEAD - 1),
+                    stop=(step == D + AHEAD - LAST - 1),
                 )
 
+        last_moduli = held.tile([N, LAST * S], F32, name="last_moduli")
+        t, d = order[D - 2]
+        nc.scalar.activation(
+            last_moduli[:, 0:S], products[D - 2][:], FUNC.Sqrt, bias=rot_norm_t[:, d : d + 1]
+        )
+        minus_sum = held.tile([N, S], F32, name="minus_sum")
+        nc.vector.scalar_tensor_tensor(
+            minus_sum[:], dist_sum[:], -1.0, last_moduli[:, 0:S], ALU.mult, ALU.subtract
+        )
+        t, d = order[D - 1]
         score = held.tile([N, S], F32, name="score")
-        nc.vector.tensor_scalar(score[:], dist_sum[:], -1.0, GAMMA, ALU.mult, ALU.add)
-        nc.sync.dma_start(out, score[:])
+        for first, queue in ((0, nc.sync), (S // 2, nc.scalar)):
+            half = slice(first, first + S // 2)
+            nc.scalar.activation(
+                last_moduli[:, S + first : S + first + S // 2],
+                products[D - 1][:, half],
+                FUNC.Sqrt,
+                bias=rot_norm_t[:, d : d + 1],
+            )
+            nc.vector.scalar_tensor_tensor(
+                score[:, half],
+                minus_sum[:, half],
+                GAMMA,
+                last_moduli[:, S + first : S + first + S // 2],
+                ALU.add,
+                ALU.subtract,
+            )
+            queue.dma_start(out[:, half], score[:, half])

@@ -6,6 +6,7 @@ from concourse.masks import make_block_diagonal, make_identity
 F32 = mybir.dt.float32
 BF16 = mybir.dt.bfloat16
 U16 = mybir.dt.uint16
+I32 = mybir.dt.int32
 ALU = mybir.AluOpType
 FUNC = mybir.ActivationFunctionType
 
@@ -35,7 +36,14 @@ def set_start(t):
 GUARD_ROOT = 1.0 + 2.0**-19
 
 AHEAD = 3
-LAST = 2
+
+PAIR = 2
+VECTOR_SETS = range(3, SETS - 3, 3)
+
+SPARED = 16
+
+SEED_MASK = 0x3FFFFFFF
+SEED_SCALE = 2.0**62.5 * 2 / (1 + math.sqrt(32 / 27))
 
 FLOPS = 7 * D * N * S
 
@@ -45,7 +53,10 @@ def tile_rotate_kernel(tc, ent, rel, offs, out):
     with (
         tc.tile_pool(name="held", bufs=1) as held,
         tc.tile_pool(name="work", bufs=AHEAD + 1) as work,
+        tc.tile_pool(name="spared", bufs=3) as spared,
+        tc.tile_pool(name="newton", bufs=1) as newton,
         tc.psum_pool(name="banks", bufs=AHEAD + 2) as banks,
+        tc.psum_pool(name="vector_banks", bufs=PAIR) as vector_banks,
         tc.psum_pool(name="once", bufs=1) as once,
     ):
         early_values = held.tile([128, 3 * CHUNK], F32, name="early_values")
@@ -56,12 +67,12 @@ def tile_rotate_kernel(tc, ent, rel, offs, out):
             )
         rel_sb = held.tile([D, N], F32, name="rel_sb")
         nc.scalar.dma_start(rel_sb[:], rel)
-        offsets = held.tile([128, N // 16], U16, name="offsets")
-        nc.sync.dma_start(offsets[:], offs)
         re_ent = held.tile([D, S], F32, name="re_ent")
-        nc.sync.dma_start(re_ent[:], ent[0:D, :])
+        nc.gpsimd.dma_start(re_ent[:], ent[0:D, :])
         im_ent = held.tile([D, S], F32, name="im_ent")
         nc.scalar.dma_start(im_ent[:], ent[D : 2 * D, :])
+        offsets = held.tile([128, N // 16], U16, name="offsets")
+        nc.sync.dma_start(offsets[:], offs)
 
         half_pi = held.tile([D, 1], F32, name="half_pi")
         nc.vector.memset(half_pi[:], math.pi / 2)
@@ -69,7 +80,7 @@ def tile_rotate_kernel(tc, ent, rel, offs, out):
         early_slots = held.tile([128, SLOTS * CHUNK], BF16, name="early_slots")
         table_slots = held.tile([D, SLOTS * S], BF16, name="table_slots")
         for b in range(3):
-            nc.gpsimd.memset(query_slots[:, (3 * b + 2) * N : (3 * b + 3) * N], 1.0)
+            nc.gpsimd.memset(query_slots[:, (3 * b + 2) * N : (3 * b + 3) * N], -0.5)
         nc.gpsimd.memset(query_slots[:, (SLOTS - 1) * N :], 0.0)
         nc.gpsimd.memset(early_slots[:, (SLOTS - 1) * CHUNK :], 0.0)
         nc.gpsimd.memset(table_slots[:, (SLOTS - 1) * S :], 0.0)
@@ -77,17 +88,19 @@ def tile_rotate_kernel(tc, ent, rel, offs, out):
         make_identity(nc, identity[:])
         own_group = held.tile([128, 128], F32, name="own_group")
         make_block_diagonal(nc, own_group[:], SLOTS)
+        nc.gpsimd.tensor_scalar(own_group[:], own_group[:], -2.0, None, ALU.mult)
         identity_bf = held.tile([N, N], BF16, name="identity_bf")
         make_identity(nc, identity_bf[:])
         table_values = held.tile([D, 3 * S], F32, name="table_values")
         for x in range(2):
             nc.gpsimd.dma_start(table_values[:, x * S : (x + 1) * S], ent[x * D : (x + 1) * D, :])
 
-        def enlarged_squares(re_part, im_part, width, name):
+        def enlarged_squares(parts, width, name):
             squares = held.tile([128, 2 * width], F32, name=name)
-            for x, part in enumerate((re_part, im_part)):
+            share = 2 * width // len(parts)
+            for x, part in enumerate(parts):
                 nc.scalar.activation(
-                    squares[:, x * width : (x + 1) * width], part, FUNC.Square, scale=GUARD_ROOT
+                    squares[:, x * share : (x + 1) * share], part, FUNC.Square, scale=GUARD_ROOT
                 )
             return squares
 
@@ -102,10 +115,10 @@ def tile_rotate_kernel(tc, ent, rel, offs, out):
         def pair(slots, width, k):
             return slots[:, k * width : (k + 2) * width]
 
-        def high_and_middle(values, rest, slots, width):
+        def high_and_middle(values, rest, slots, width, cast_middle):
             nc.vector.tensor_copy(piece(slots, width, 0), values[:])
             nc.vector.tensor_tensor(rest[:], values[:], piece(slots, width, 0), ALU.subtract)
-            nc.vector.tensor_copy(piece(slots, width, 1), rest[:])
+            cast_middle(piece(slots, width, 1), rest[:])
 
         def low(rest, slots, width):
             nc.vector.tensor_tensor(
@@ -116,46 +129,38 @@ def tile_rotate_kernel(tc, ent, rel, offs, out):
             for i, (a, b) in enumerate(REPEATS):
                 copy(pair(slots, width, REPEAT_SLOT + 2 * i), pair(slots, width, 3 * b))
 
-        early_sq = enlarged_squares(
-            early_values[:, 0:CHUNK], early_values[:, CHUNK : 2 * CHUNK], CHUNK, "early_sq"
-        )
+        early_sq = enlarged_squares([early_values[:, 0 : 2 * CHUNK]], CHUNK, "early_sq")
         add_squares(early_values, early_sq, CHUNK)
-        early_rest = held.tile([128, 3 * CHUNK], F32, name="early_rest")
-        high_and_middle(early_values, early_rest, early_slots, CHUNK)
-        low(early_rest, early_slots, CHUNK)
-        trig = held.tile([D, 2 * N], F32, name="trig")
-        nc.scalar.activation(trig[:, N : 2 * N], rel_sb[:], FUNC.Sin, scale=PHASE_PER_REL)
+        sin_ph = held.tile([D, N], F32, name="sin_ph")
+        nc.scalar.activation(sin_ph[:], rel_sb[:], FUNC.Sin, scale=PHASE_PER_REL)
+        minus_sin = held.tile([D, N], F32, name="minus_sin")
+        nc.scalar.activation(minus_sin[:], rel_sb[:], FUNC.Sin, scale=-PHASE_PER_REL)
         abs_rel = held.tile([D, N], F32, name="abs_rel")
         nc.scalar.activation(abs_rel[:], rel_sb[:], FUNC.Abs)
-        nc.scalar.activation(
-            trig[:, 0:N], abs_rel[:], FUNC.Sin, bias=half_pi[:], scale=-PHASE_PER_REL
-        )
-        twice = held.tile([D, 2 * N], F32, name="twice")
-        nc.scalar.mul(twice[:], trig[:], -2.0)
-        cos2 = twice[:, 0:N]
-        sin2 = twice[:, N : 2 * N]
+        cos_ph = held.tile([D, N], F32, name="cos_ph")
+        nc.scalar.activation(cos_ph[:], abs_rel[:], FUNC.Sin, bias=half_pi[:], scale=-PHASE_PER_REL)
+        early_rest = held.tile([128, 3 * CHUNK], F32, name="early_rest")
+        high_and_middle(early_values, early_rest, early_slots, CHUNK, nc.scalar.copy)
         repeats(early_slots, CHUNK, nc.scalar.copy)
-        table_sq = enlarged_squares(re_ent[:], im_ent[:], S, "table_sq")
+        table_sq = enlarged_squares([re_ent[:], im_ent[:]], S, "table_sq")
 
-        re_cos = held.tile([D, N], F32, name="re_cos")
-        nc.vector.tensor_tensor(re_cos[:], re_ent[:].indirect(offsets[:]), cos2, ALU.mult)
-        im_sin = held.tile([D, N], F32, name="im_sin")
-        nc.vector.tensor_tensor(im_sin[:], im_ent[:].indirect(offsets[:]), sin2, ALU.mult)
-        re_sin = held.tile([D, N], F32, name="re_sin")
-        nc.vector.tensor_tensor(re_sin[:], re_ent[:].indirect(offsets[:]), sin2, ALU.mult)
-        im_cos = held.tile([D, N], F32, name="im_cos")
-        nc.vector.tensor_tensor(im_cos[:], im_ent[:].indirect(offsets[:]), cos2, ALU.mult)
-        query = held.tile([D, 2 * N], F32, name="query")
-        nc.vector.tensor_tensor(query[:, 0:N], re_cos[:], im_sin[:], ALU.subtract)
-        nc.vector.tensor_tensor(query[:, N : 2 * N], re_sin[:], im_cos[:], ALU.add)
+        from_re = held.tile([D, 2 * N], F32, name="from_re")
+        from_im = held.tile([D, 2 * N], F32, name="from_im")
+        nc.vector.tensor_tensor(from_re[:, 0:N], re_ent[:].indirect(offsets[:]), cos_ph[:], ALU.mult)
+        nc.vector.tensor_tensor(from_im[:, 0:N], im_ent[:].indirect(offsets[:]), minus_sin[:], ALU.mult)
+        nc.vector.tensor_tensor(from_re[:, N:], re_ent[:].indirect(offsets[:]), sin_ph[:], ALU.mult)
+        nc.vector.tensor_tensor(from_im[:, N:], im_ent[:].indirect(offsets[:]), cos_ph[:], ALU.mult)
+        low(early_rest, early_slots, CHUNK)
+        rot = held.tile([D, 2 * N], F32, name="rot")
+        nc.vector.tensor_tensor(rot[:], from_re[:], from_im[:], ALU.add)
 
         homes = [[3 * b for b in range(3)], [], []]
         for i, (a, b) in enumerate(REPEATS):
             homes[a].append(REPEAT_SLOT + 2 * i)
         query_rest = held.tile([D, 2 * N], F32, name="query_rest")
-        nc.vector.tensor_copy(pair(query_slots, N, homes[0][0]), query[:])
+        nc.vector.tensor_tensor(pair(query_slots, N, homes[0][0]), from_re[:], from_im[:], ALU.add)
         nc.vector.tensor_tensor(
-            query_rest[:], query[:], pair(query_slots, N, homes[0][0]), ALU.subtract
+            query_rest[:], rot[:], pair(query_slots, N, homes[0][0]), ALU.subtract
         )
         nc.vector.tensor_copy(pair(query_slots, N, homes[1][0]), query_rest[:])
         nc.vector.tensor_tensor(
@@ -166,13 +171,13 @@ def tile_rotate_kernel(tc, ent, rel, offs, out):
         )
 
         rot_sq = held.tile([D, 2 * N], F32, name="rot_sq")
-        nc.scalar.activation(rot_sq[:], query[:], FUNC.Square, scale=GUARD_ROOT / 2)
+        nc.scalar.activation(rot_sq[:], rot[:], FUNC.Square, scale=GUARD_ROOT)
         for slots_of_piece in homes:
             for k in slots_of_piece[1:]:
                 nc.scalar.copy(pair(query_slots, N, k), pair(query_slots, N, slots_of_piece[0]))
         rot_norm = held.tile([D, N], F32, name="rot_norm")
         nc.vector.tensor_tensor(rot_norm[:], rot_sq[:, 0:N], rot_sq[:, N : 2 * N], ALU.add)
-        rot_norm_ps = once.tile([N, D], F32, name="rot_norm_ps")
+        rot_norm_ps = vector_banks.tile([N, D], F32, name="rot_norm_ps", tag="vector_product")
         nc.tensor.transpose(rot_norm_ps[:], rot_norm[:], identity[:])
         rot_norm_t = held.tile([N, D], F32, name="rot_norm_t")
         nc.scalar.copy(rot_norm_t[:], rot_norm_ps[:])
@@ -218,22 +223,83 @@ def tile_rotate_kernel(tc, ent, rel, offs, out):
         make_weights(1, APART - 1)
         add_squares(table_values, table_sq, S)
         table_rest = held.tile([D, 3 * S], F32, name="table_rest")
-        high_and_middle(table_values, table_rest, table_slots, S)
+        high_and_middle(table_values, table_rest, table_slots, S, nc.vector.tensor_copy)
         low(table_rest, table_slots, S)
         repeats(table_slots, S, nc.vector.tensor_copy)
-        for first in range(APART, SETS, APART):
+
+        def prepare(first):
             for t in range(first, first + APART):
                 collect(query_rows, query_slots, N, t)
             for t in range(first, first + APART):
                 collect(table_rows, table_slots, S, t)
             make_weights(first, APART)
 
-        order = [(t, set_start(t) + APART * g) for t in range(SETS) for g in range(GROUPS)]
+        prepare(APART)
+
+        vector_sum = held.tile([N, PAIR * S], F32, name="vector_sum")
+        nc.gpsimd.memset(vector_sum[:, 0:S], -GAMMA)
+        nc.gpsimd.memset(vector_sum[:, S:], 0.0)
+        vector_total = held.tile([N, S], F32, name="vector_total")
+
+        def vector_roots(t):
+            wide = [N, PAIR * S]
+            value = newton.tile(wide, F32, name="value")
+            for i in range(PAIR):
+                d = set_start(t) + APART * i
+                product = vector_banks.tile([N, S], F32, name="product", tag="vector_product")
+                nc.tensor.matmul(
+                    product[:],
+                    weights[:, d * N : (d + 1) * N],
+                    table_rows[:, t * S : (t + 1) * S],
+                    start=True,
+                    stop=True,
+                )
+                nc.vector.tensor_scalar(
+                    value[:, i * S : (i + 1) * S], product[:], rot_norm_t[:, d : d + 1], None, ALU.add
+                )
+            seed = newton.tile(wide, I32, name="seed")
+            nc.vector.tensor_scalar(
+                seed[:], value[:].bitcast(I32), 1, SEED_MASK, ALU.logical_shift_right, ALU.bitwise_xor
+            )
+            guess = seed[:].bitcast(F32)
+            x_guess = newton.tile(wide, F32, name="x_guess")
+            nc.vector.tensor_tensor(x_guess[:], value[:], guess, ALU.mult)
+            minus_half = newton.tile(wide, F32, name="minus_half")
+            nc.vector.scalar_tensor_tensor(
+                minus_half[:], x_guess[:], -0.5 * SEED_SCALE**2, guess, ALU.mult, ALU.mult
+            )
+            better = newton.tile(wide, F32, name="better")
+            nc.vector.scalar_tensor_tensor(better[:], minus_half[:], 1.5, guess, ALU.add, ALU.mult)
+            root = newton.tile(wide, F32, name="root")
+            nc.vector.scalar_tensor_tensor(root[:], better[:], SEED_SCALE, value[:], ALU.mult, ALU.mult)
+            minus_half_2 = newton.tile(wide, F32, name="minus_half_2")
+            nc.vector.scalar_tensor_tensor(
+                minus_half_2[:], root[:], -0.5 * SEED_SCALE, better[:], ALU.mult, ALU.mult
+            )
+            vector_modulus = newton.tile(wide, F32, name="vector_modulus")
+            nc.vector.scalar_tensor_tensor(
+                vector_modulus[:], minus_half_2[:], 1.5, root[:], ALU.add, ALU.mult
+            )
+            nc.vector.tensor_tensor(vector_sum[:], vector_sum[:], vector_modulus[:], ALU.add)
+
+        order = [
+            (t, g)
+            for t in range(SETS)
+            for g in range(GROUPS)
+            if not (t in VECTOR_SETS and g < PAIR)
+        ]
+        count = len(order)
         dist_sum = once.tile([N, S], F32, name="dist_sum")
         products = []
-        for step in range(D + AHEAD - LAST):
-            if step < D:
-                t, d = order[step]
+        for step in range(count + AHEAD):
+            if step < count:
+                t, g = order[step]
+                d = set_start(t) + APART * g
+                if t in VECTOR_SETS and g == PAIR:
+                    vector_roots(t)
+                    missing = APART * (VECTOR_SETS.index(t) + 2)
+                    if missing < SETS:
+                        prepare(missing)
                 mod_sq = banks.tile([N, S], F32, name="mod_sq")
                 nc.tensor.matmul(
                     mod_sq[:],
@@ -244,44 +310,35 @@ def tile_rotate_kernel(tc, ent, rel, offs, out):
                 )
                 products.append(mod_sq)
             if step >= AHEAD:
-                t, d = order[step - AHEAD]
-                modulus = work.tile([N, S], BF16, name="modulus")
-                nc.scalar.activation(
-                    modulus[:], products[step - AHEAD][:], FUNC.Sqrt, bias=rot_norm_t[:, d : d + 1]
-                )
-                nc.tensor.matmul(
-                    dist_sum[:],
-                    identity_bf[:],
-                    modulus[:],
-                    start=(step == AHEAD),
-                    stop=(step == D + AHEAD - LAST - 1),
-                )
+                t, g = order[step - AHEAD]
+                d = set_start(t) + APART * g
+                if (step - AHEAD) % SPARED == SPARED // 2:
+                    spared_modulus = spared.tile([N, S], F32, name="spared_modulus")
+                    nc.scalar.activation(
+                        spared_modulus[:],
+                        products[step - AHEAD][:],
+                        FUNC.Sqrt,
+                        bias=rot_norm_t[:, d : d + 1],
+                    )
+                    nc.vector.tensor_tensor(
+                        vector_sum[:, 0:S], vector_sum[:, 0:S], spared_modulus[:], ALU.add
+                    )
+                else:
+                    modulus = work.tile([N, S], BF16, name="modulus")
+                    nc.scalar.activation(
+                        modulus[:], products[step - AHEAD][:], FUNC.Sqrt, bias=rot_norm_t[:, d : d + 1]
+                    )
+                    nc.tensor.matmul(
+                        dist_sum[:],
+                        identity_bf[:],
+                        modulus[:],
+                        start=(step == AHEAD),
+                        stop=(step == count + AHEAD - 1),
+                    )
 
-        last_moduli = held.tile([N, LAST * S], F32, name="last_moduli")
-        t, d = order[D - 2]
-        nc.scalar.activation(
-            last_moduli[:, 0:S], products[D - 2][:], FUNC.Sqrt, bias=rot_norm_t[:, d : d + 1]
-        )
-        minus_sum = held.tile([N, S], F32, name="minus_sum")
-        nc.vector.scalar_tensor_tensor(
-            minus_sum[:], dist_sum[:], -1.0, last_moduli[:, 0:S], ALU.mult, ALU.subtract
-        )
-        t, d = order[D - 1]
+        nc.vector.tensor_tensor(vector_total[:], vector_sum[:, 0:S], vector_sum[:, S:], ALU.add)
         score = held.tile([N, S], F32, name="score")
-        for first, queue in ((0, nc.sync), (S // 2, nc.scalar)):
-            half = slice(first, first + S // 2)
-            nc.scalar.activation(
-                last_moduli[:, S + first : S + first + S // 2],
-                products[D - 1][:, half],
-                FUNC.Sqrt,
-                bias=rot_norm_t[:, d : d + 1],
-            )
-            nc.vector.scalar_tensor_tensor(
-                score[:, half],
-                minus_sum[:, half],
-                GAMMA,
-                last_moduli[:, S + first : S + first + S // 2],
-                ALU.add,
-                ALU.subtract,
-            )
-            queue.dma_start(out[:, half], score[:, half])
+        nc.vector.scalar_tensor_tensor(
+            score[:], dist_sum[:], -1.0, vector_total[:], ALU.mult, ALU.subtract
+        )
+        nc.sync.dma_start(out, score[:])

@@ -35,7 +35,7 @@ def set_start(t):
 
 GUARD_ROOT = 1.0 + 2.0**-19
 
-AHEAD = 3
+AHEAD = 4
 
 PAIR = 2
 VECTOR_SETS = range(3, SETS - 3, 3)
@@ -55,7 +55,7 @@ def tile_rotate_kernel(tc, ent, rel, offs, out):
         tc.tile_pool(name="work", bufs=AHEAD + 1) as work,
         tc.tile_pool(name="spared", bufs=3) as spared,
         tc.tile_pool(name="newton", bufs=1) as newton,
-        tc.psum_pool(name="banks", bufs=AHEAD + 2) as banks,
+        tc.psum_pool(name="banks", bufs=AHEAD + 1) as banks,
         tc.psum_pool(name="vector_banks", bufs=PAIR) as vector_banks,
         tc.psum_pool(name="once", bufs=1) as once,
     ):

@@ -60,22 +60,25 @@ def tile_rotate_kernel(tc, ent, rel, offs, out):
         tc.psum_pool(name="once", bufs=1) as once,
     ):
         early_values = held.tile([128, 3 * CHUNK], F32, name="early_values")
-        for x in range(2):
-            nc.sync.dma_start(
-                early_values[:, x * CHUNK : (x + 1) * CHUNK],
-                ent[x * D : x * D + SPAN, :].rearrange("d (c y) -> (d c) y", y=CHUNK),
-            )
+        nc.sync.dma_start(
+            early_values[:, 0 : 2 * CHUNK].rearrange("p (x y) -> p x y", x=2),
+            ent.rearrange("(x d) (c y) -> x d c y", x=2, y=CHUNK)[:, 0:SPAN].rearrange(
+                "x d c y -> (d c) x y"
+            ),
+        )
         rel_sb = held.tile([D, N], F32, name="rel_sb")
         nc.scalar.dma_start(rel_sb[:], rel)
-        re_ent = held.tile([D, S], F32, name="re_ent")
-        nc.gpsimd.dma_start(re_ent[:], ent[0:D, :])
         im_ent = held.tile([D, S], F32, name="im_ent")
         nc.scalar.dma_start(im_ent[:], ent[D : 2 * D, :])
         offsets = held.tile([128, N // 16], U16, name="offsets")
         nc.sync.dma_start(offsets[:], offs)
+        re_ent = held.tile([D, S], F32, name="re_ent")
+        nc.sync.dma_start(re_ent[:], ent[0:D, :])
 
         half_pi = held.tile([D, 1], F32, name="half_pi")
         nc.vector.memset(half_pi[:], math.pi / 2)
+        warm_up = held.tile([D, 1], F32, name="warm_up")
+        nc.scalar.activation(warm_up[:], half_pi[:], FUNC.Sin)
         query_slots = held.tile([D, SLOTS * N], BF16, name="query_slots")
         early_slots = held.tile([128, SLOTS * CHUNK], BF16, name="early_slots")
         table_slots = held.tile([D, SLOTS * S], BF16, name="table_slots")
@@ -181,6 +184,8 @@ def tile_rotate_kernel(tc, ent, rel, offs, out):
         nc.tensor.transpose(rot_norm_ps[:], rot_norm[:], identity[:])
         rot_norm_t = held.tile([N, D], F32, name="rot_norm_t")
         nc.scalar.copy(rot_norm_t[:], rot_norm_ps[:])
+        warm_up_root = held.tile([N, 1], F32, name="warm_up_root")
+        nc.scalar.activation(warm_up_root[:], rot_norm_t[:, 0:1], FUNC.Sqrt)
 
         query_rows = held.tile([128, SETS * N], BF16, name="query_rows")
         table_rows = held.tile([128, SETS * S], BF16, name="table_rows")

@@ -40,7 +40,7 @@ AHEAD = 4
 PAIR = 2
 VECTOR_SETS = range(3, SETS - 3, 3)
 
-SPARED = 16
+SPARED = 12
 
 SEED_MASK = 0x3FFFFFFF
 SEED_SCALE = 2.0**62.5 * 2 / (1 + math.sqrt(32 / 27))
@@ -53,7 +53,7 @@ def tile_rotate_kernel(tc, ent, rel, offs, out):
     with (
         tc.tile_pool(name="held", bufs=1) as held,
         tc.tile_pool(name="work", bufs=AHEAD + 1) as work,
-        tc.tile_pool(name="spared", bufs=3) as spared,
+        tc.tile_pool(name="spared", bufs=4) as spared,
         tc.tile_pool(name="newton", bufs=1) as newton,
         tc.psum_pool(name="banks", bufs=AHEAD + 1) as banks,
         tc.psum_pool(name="vector_banks", bufs=PAIR) as vector_banks,
@@ -317,7 +317,7 @@ def tile_rotate_kernel(tc, ent, rel, offs, out):
             if step >= AHEAD:
                 t, g = order[step - AHEAD]
                 d = set_start(t) + APART * g
-                if (step - AHEAD) % SPARED == SPARED // 2:
+                if (step - AHEAD) % SPARED == SPARED // 2 and step - AHEAD < count - GROUPS:
                     spared_modulus = spared.tile([N, S], F32, name="spared_modulus")
                     nc.scalar.activation(
                         spared_modulus[:],

@@ -1,7 +1,7 @@
 import math
 
 import concourse.mybir as mybir
-from concourse.masks import make_block_diagonal, make_identity
+from concourse.masks import make_identity
 
 F32 = mybir.dt.float32
 BF16 = mybir.dt.bfloat16
@@ -38,12 +38,26 @@ GUARD_ROOT = 1.0 + 2.0**-19
 AHEAD = 4
 
 PAIR = 2
-VECTOR_SETS = range(3, SETS - 3, 3)
+VECTOR_SETS = range(2, SETS - 3, 2)
 
 SPARED = 12
 
-SEED_MASK = 0x3FFFFFFF
-SEED_SCALE = 2.0**62.5 * 2 / (1 + math.sqrt(32 / 27))
+SIGMA = 1 - (1 + math.log(math.log(2))) / math.log(2)
+SEED = 1.5 * (127 - SIGMA) * 2.0**23
+U_LOW, U_HIGH = 0.8708, 0.9872
+
+
+def inverse_root_polynomial(low, high):
+    u = [(low + high) / 2 + (high - low) / 2 * math.cos(math.pi * (2 * k + 1) / 6) for k in range(3)]
+    f = [v**-0.5 for v in u]
+    slope = (f[1] - f[0]) / (u[1] - u[0])
+    c2 = ((f[2] - f[1]) / (u[2] - u[1]) - slope) / (u[2] - u[0])
+    c1 = slope - c2 * (u[0] + u[1])
+    return f[0] - u[0] * (c1 + c2 * u[0]), c1, c2
+
+
+C0, C1, C2 = inverse_root_polynomial(U_LOW, U_HIGH)
+A = C2 ** (1 / 3)
 
 FLOPS = 7 * D * N * S
 
@@ -54,7 +68,7 @@ def tile_rotate_kernel(tc, ent, rel, offs, out):
         tc.tile_pool(name="held", bufs=1) as held,
         tc.tile_pool(name="work", bufs=AHEAD + 1) as work,
         tc.tile_pool(name="spared", bufs=4) as spared,
-        tc.tile_pool(name="newton", bufs=1) as newton,
+        tc.tile_pool(name="root_work", bufs=1) as root_work,
         tc.psum_pool(name="banks", bufs=AHEAD + 1) as banks,
         tc.psum_pool(name="vector_banks", bufs=PAIR) as vector_banks,
         tc.psum_pool(name="once", bufs=1) as once,
@@ -89,22 +103,49 @@ def tile_rotate_kernel(tc, ent, rel, offs, out):
         nc.gpsimd.memset(table_slots[:, (SLOTS - 1) * S :], 0.0)
         identity = held.tile([D, D], F32, name="identity")
         make_identity(nc, identity[:])
-        own_group = held.tile([128, 128], F32, name="own_group")
-        make_block_diagonal(nc, own_group[:], SLOTS)
-        nc.gpsimd.tensor_scalar(own_group[:], own_group[:], -2.0, None, ALU.mult)
-        identity_bf = held.tile([N, N], BF16, name="identity_bf")
-        make_identity(nc, identity_bf[:])
+        pick = held.tile([D, 128 + SLOTS], BF16, name="pick")
+        nc.gpsimd.memset(pick[:], 0.0)
+        nc.gpsimd.tensor_copy(pick[:, SLOTS - 1 : 128 : SLOTS], identity[:, 0:SPAN:APART])
+        own_group = held.tile([128, GROUPS], F32, name="own_group")
+        nc.gpsimd.memset(own_group[:], 0.0)
+        for compare, fill, base in ((ALU.is_gt, -2.0, 1 - SLOTS), (ALU.is_ge, 0.0, 0)):
+            nc.gpsimd.affine_select(
+                out=own_group[:],
+                in_=own_group[:],
+                compare_op=compare,
+                fill=fill,
+                base=base,
+                pattern=[[-SLOTS, GROUPS]],
+                channel_multiplier=1,
+            )
         table_values = held.tile([D, 3 * S], F32, name="table_values")
         for x in range(2):
             nc.gpsimd.dma_start(table_values[:, x * S : (x + 1) * S], ent[x * D : (x + 1) * D, :])
+        identity_bf = held.tile([N, N], BF16, name="identity_bf")
+        make_identity(nc, identity_bf[:])
 
-        def enlarged_squares(parts, width, name):
-            squares = held.tile([128, 2 * width], F32, name=name)
-            share = 2 * width // len(parts)
-            for x, part in enumerate(parts):
-                nc.scalar.activation(
-                    squares[:, x * share : (x + 1) * share], part, FUNC.Square, scale=GUARD_ROOT
+        query_rows = held.tile([128, SETS * N], BF16, name="query_rows")
+        table_rows = held.tile([128, SETS * S], BF16, name="table_rows")
+
+        def collect(rows, slots, width, t):
+            last = set_start(t) + APART * (GROUPS - 1)
+            nc.sync.dma_start(
+                rows[:, t * width : (t + 1) * width], slots[set_start(t) : last + 1 : APART, :]
+            )
+
+        def collect_early(t):
+            for c in range(PARTS):
+                first = PARTS * set_start(t) + c
+                last = first + PARTS * APART * (GROUPS - 1)
+                queue = nc.scalar if t == 0 and c % 2 == 1 else nc.sync
+                queue.dma_start(
+                    table_rows[:, t * S + c * CHUNK : t * S + (c + 1) * CHUNK],
+                    early_slots[first : last + 1 : PARTS * APART, :],
                 )
+
+        def enlarged_squares(values, width, name):
+            squares = held.tile([128, 2 * width], F32, name=name)
+            nc.scalar.activation(squares[:], values[:, 0 : 2 * width], FUNC.Square, scale=GUARD_ROOT)
             return squares
 
         def add_squares(values, squares, width):
@@ -132,7 +173,7 @@ def tile_rotate_kernel(tc, ent, rel, offs, out):
             for i, (a, b) in enumerate(REPEATS):
                 copy(pair(slots, width, REPEAT_SLOT + 2 * i), pair(slots, width, 3 * b))
 
-        early_sq = enlarged_squares([early_values[:, 0 : 2 * CHUNK]], CHUNK, "early_sq")
+        early_sq = enlarged_squares(early_values, CHUNK, "early_sq")
         add_squares(early_values, early_sq, CHUNK)
         sin_ph = held.tile([D, N], F32, name="sin_ph")
         nc.scalar.activation(sin_ph[:], rel_sb[:], FUNC.Sin, scale=PHASE_PER_REL)
@@ -145,7 +186,6 @@ def tile_rotate_kernel(tc, ent, rel, offs, out):
         early_rest = held.tile([128, 3 * CHUNK], F32, name="early_rest")
         high_and_middle(early_values, early_rest, early_slots, CHUNK, nc.scalar.copy)
         repeats(early_slots, CHUNK, nc.scalar.copy)
-        table_sq = enlarged_squares([re_ent[:], im_ent[:]], S, "table_sq")
 
         from_re = held.tile([D, 2 * N], F32, name="from_re")
         from_im = held.tile([D, 2 * N], F32, name="from_im")
@@ -154,6 +194,7 @@ def tile_rotate_kernel(tc, ent, rel, offs, out):
         nc.vector.tensor_tensor(from_re[:, N:], re_ent[:].indirect(offsets[:]), sin_ph[:], ALU.mult)
         nc.vector.tensor_tensor(from_im[:, N:], im_ent[:].indirect(offsets[:]), cos_ph[:], ALU.mult)
         low(early_rest, early_slots, CHUNK)
+        collect_early(0)
         rot = held.tile([D, 2 * N], F32, name="rot")
         nc.vector.tensor_tensor(rot[:], from_re[:], from_im[:], ALU.add)
 
@@ -173,59 +214,57 @@ def tile_rotate_kernel(tc, ent, rel, offs, out):
             ALU.subtract,
         )
 
-        rot_sq = held.tile([D, 2 * N], F32, name="rot_sq")
-        nc.scalar.activation(rot_sq[:], rot[:], FUNC.Square, scale=GUARD_ROOT)
+        source = list(range(SLOTS - 1))
         for slots_of_piece in homes:
             for k in slots_of_piece[1:]:
-                nc.scalar.copy(pair(query_slots, N, k), pair(query_slots, N, slots_of_piece[0]))
+                for x in range(2):
+                    source[k + x] = slots_of_piece[0] + x
+        by_piece = sorted(range(SLOTS - 1), key=lambda k: source[k])
+        first_rows = vector_banks.tile([128, N], F32, name="first_rows", tag="vector_product")
+        for k in by_piece:
+            nc.tensor.matmul(
+                first_rows[:],
+                pick[:, SLOTS - 1 - k : SLOTS - 1 - k + 128],
+                query_slots[:, source[k] * N : (source[k] + 1) * N],
+                start=(k == by_piece[0]),
+                stop=(k == by_piece[-1]),
+            )
+
+        rot_sq = held.tile([D, 2 * N], F32, name="rot_sq")
+        nc.scalar.activation(rot_sq[:], rot[:], FUNC.Square, scale=GUARD_ROOT)
+        warm_up_root = held.tile([D, 1], F32, name="warm_up_root")
+        nc.scalar.activation(warm_up_root[:], rot_sq[:, 0:1], FUNC.Sqrt)
+        for slots_of_piece in homes:
+            for k in slots_of_piece[1:]:
+                nc.vector.tensor_copy(pair(query_slots, N, k), pair(query_slots, N, slots_of_piece[0]))
         rot_norm = held.tile([D, N], F32, name="rot_norm")
         nc.vector.tensor_tensor(rot_norm[:], rot_sq[:, 0:N], rot_sq[:, N : 2 * N], ALU.add)
         rot_norm_ps = vector_banks.tile([N, D], F32, name="rot_norm_ps", tag="vector_product")
         nc.tensor.transpose(rot_norm_ps[:], rot_norm[:], identity[:])
         rot_norm_t = held.tile([N, D], F32, name="rot_norm_t")
         nc.scalar.copy(rot_norm_t[:], rot_norm_ps[:])
-        warm_up_root = held.tile([N, 1], F32, name="warm_up_root")
-        nc.scalar.activation(warm_up_root[:], rot_norm_t[:, 0:1], FUNC.Sqrt)
-
-        query_rows = held.tile([128, SETS * N], BF16, name="query_rows")
-        table_rows = held.tile([128, SETS * S], BF16, name="table_rows")
-
-        def collect(rows, slots, width, t):
-            last = set_start(t) + APART * (GROUPS - 1)
-            nc.sync.dma_start(
-                rows[:, t * width : (t + 1) * width], slots[set_start(t) : last + 1 : APART, :]
-            )
-
-        def collect_early(t):
-            for c in range(PARTS):
-                first = PARTS * set_start(t) + c
-                last = first + PARTS * APART * (GROUPS - 1)
-                nc.sync.dma_start(
-                    table_rows[:, t * S + c * CHUNK : t * S + (c + 1) * CHUNK],
-                    early_slots[first : last + 1 : PARTS * APART, :],
-                )
-
-        collect_early(0)
-        for t in range(APART):
-            collect(query_rows, query_slots, N, t)
+        collect_early(1)
         for t in range(1, APART):
+            collect(query_rows, query_slots, N, t)
+        for t in range(2, APART):
             collect_early(t)
 
         weights = held.tile([128, D * N], BF16, name="weights")
 
-        def make_weights(t, count):
+        def make_weights(rows, t, count):
             for g in range(GROUPS):
                 d = set_start(t) + APART * g
                 nc.vector.tensor_scalar(
                     weights[:, d * N : (d + count) * N],
-                    query_rows[:, t * N : (t + count) * N],
-                    own_group[:, SLOTS * g : SLOTS * g + 1],
+                    rows,
+                    own_group[:, g : g + 1],
                     None,
                     ALU.mult,
                 )
 
-        make_weights(0, 1)
-        make_weights(1, APART - 1)
+        make_weights(first_rows[:], 0, 1)
+        make_weights(query_rows[:, N : APART * N], 1, APART - 1)
+        table_sq = enlarged_squares(table_values, S, "table_sq")
         add_squares(table_values, table_sq, S)
         table_rest = held.tile([D, 3 * S], F32, name="table_rest")
         high_and_middle(table_values, table_rest, table_slots, S, nc.vector.tensor_copy)
@@ -237,7 +276,7 @@ def tile_rotate_kernel(tc, ent, rel, offs, out):
                 collect(query_rows, query_slots, N, t)
             for t in range(first, first + APART):
                 collect(table_rows, table_slots, S, t)
-            make_weights(first, APART)
+            make_weights(query_rows[:, first * N : (first + APART) * N], first, APART)
 
         prepare(APART)
 
@@ -248,7 +287,7 @@ def tile_rotate_kernel(tc, ent, rel, offs, out):
 
         def vector_roots(t):
             wide = [N, PAIR * S]
-            value = newton.tile(wide, F32, name="value")
+            value = root_work.tile(wide, F32, name="value")
             for i in range(PAIR):
                 d = set_start(t) + APART * i
                 product = vector_banks.tile([N, S], F32, name="product", tag="vector_product")
@@ -262,28 +301,18 @@ def tile_rotate_kernel(tc, ent, rel, offs, out):
                 nc.vector.tensor_scalar(
                     value[:, i * S : (i + 1) * S], product[:], rot_norm_t[:, d : d + 1], None, ALU.add
                 )
-            seed = newton.tile(wide, I32, name="seed")
-            nc.vector.tensor_scalar(
-                seed[:], value[:].bitcast(I32), 1, SEED_MASK, ALU.logical_shift_right, ALU.bitwise_xor
-            )
+            seed = root_work.tile(wide, I32, name="seed")
+            nc.vector.tensor_scalar(seed[:], value[:].bitcast(I32), -0.5, SEED, ALU.mult, ALU.add)
             guess = seed[:].bitcast(F32)
-            x_guess = newton.tile(wide, F32, name="x_guess")
-            nc.vector.tensor_tensor(x_guess[:], value[:], guess, ALU.mult)
-            minus_half = newton.tile(wide, F32, name="minus_half")
+            a = root_work.tile(wide, F32, name="a")
+            nc.vector.scalar_tensor_tensor(a[:], value[:], A, guess, ALU.mult, ALU.mult)
+            b = root_work.tile(wide, F32, name="b")
+            nc.vector.tensor_tensor(b[:], a[:], guess, ALU.mult)
+            parabola = root_work.tile(wide, F32, name="parabola")
+            nc.vector.scalar_tensor_tensor(parabola[:], b[:], C1 / A**2, b[:], ALU.add, ALU.mult)
+            vector_modulus = root_work.tile(wide, F32, name="vector_modulus")
             nc.vector.scalar_tensor_tensor(
-                minus_half[:], x_guess[:], -0.5 * SEED_SCALE**2, guess, ALU.mult, ALU.mult
-            )
-            better = newton.tile(wide, F32, name="better")
-            nc.vector.scalar_tensor_tensor(better[:], minus_half[:], 1.5, guess, ALU.add, ALU.mult)
-            root = newton.tile(wide, F32, name="root")
-            nc.vector.scalar_tensor_tensor(root[:], better[:], SEED_SCALE, value[:], ALU.mult, ALU.mult)
-            minus_half_2 = newton.tile(wide, F32, name="minus_half_2")
-            nc.vector.scalar_tensor_tensor(
-                minus_half_2[:], root[:], -0.5 * SEED_SCALE, better[:], ALU.mult, ALU.mult
-            )
-            vector_modulus = newton.tile(wide, F32, name="vector_modulus")
-            nc.vector.scalar_tensor_tensor(
-                vector_modulus[:], minus_half_2[:], 1.5, root[:], ALU.add, ALU.mult
+                vector_modulus[:], parabola[:], C0 / A, a[:], ALU.add, ALU.mult
             )
             nc.vector.tensor_tensor(vector_sum[:], vector_sum[:], vector_modulus[:], ALU.add)
 

@@ -40,7 +40,7 @@ AHEAD = 4
 PAIR = 2
 VECTOR_SETS = range(2, SETS - 3, 2)
 
-SPARED = 12
+SPARED = 8
 
 SIGMA = 1 - (1 + math.log(math.log(2))) / math.log(2)
 SEED = 1.5 * (127 - SIGMA) * 2.0**23
@@ -67,7 +67,7 @@ def tile_rotate_kernel(tc, ent, rel, offs, out):
     with (
         tc.tile_pool(name="held", bufs=1) as held,
         tc.tile_pool(name="work", bufs=AHEAD + 1) as work,
-        tc.tile_pool(name="spared", bufs=4) as spared,
+        tc.tile_pool(name="spared", bufs=6) as spared,
         tc.tile_pool(name="root_work", bufs=1) as root_work,
         tc.psum_pool(name="banks", bufs=AHEAD + 1) as banks,
         tc.psum_pool(name="vector_banks", bufs=PAIR) as vector_banks,
@@ -143,28 +143,16 @@ def tile_rotate_kernel(tc, ent, rel, offs, out):
                     early_slots[first : last + 1 : PARTS * APART, :],
                 )
 
-        def enlarged_squares(values, width, name):
-            squares = held.tile([128, 2 * width], F32, name=name)
-            nc.scalar.activation(squares[:], values[:, 0 : 2 * width], FUNC.Square, scale=GUARD_ROOT)
-            return squares
-
-        def add_squares(values, squares, width):
-            nc.vector.tensor_tensor(
-                values[:, 2 * width :], squares[:, 0:width], squares[:, width:], ALU.add
-            )
-
         def piece(slots, width, b):
             return slots[:, 3 * b * width : 3 * (b + 1) * width]
 
         def pair(slots, width, k):
             return slots[:, k * width : (k + 2) * width]
 
-        def high_and_middle(values, rest, slots, width, cast_middle):
+        def split(values, rest, slots, width):
             nc.vector.tensor_copy(piece(slots, width, 0), values[:])
             nc.vector.tensor_tensor(rest[:], values[:], piece(slots, width, 0), ALU.subtract)
-            cast_middle(piece(slots, width, 1), rest[:])
-
-        def low(rest, slots, width):
+            nc.vector.tensor_copy(piece(slots, width, 1), rest[:])
             nc.vector.tensor_tensor(
                 piece(slots, width, 2), rest[:], piece(slots, width, 1), ALU.subtract
             )
@@ -173,8 +161,13 @@ def tile_rotate_kernel(tc, ent, rel, offs, out):
             for i, (a, b) in enumerate(REPEATS):
                 copy(pair(slots, width, REPEAT_SLOT + 2 * i), pair(slots, width, 3 * b))
 
-        early_sq = enlarged_squares(early_values, CHUNK, "early_sq")
-        add_squares(early_values, early_sq, CHUNK)
+        early_sq = held.tile([128, 2 * CHUNK], F32, name="early_sq")
+        nc.scalar.activation(
+            early_sq[:], early_values[:, 0 : 2 * CHUNK], FUNC.Square, scale=GUARD_ROOT
+        )
+        nc.vector.tensor_tensor(
+            early_values[:, 2 * CHUNK :], early_sq[:, 0:CHUNK], early_sq[:, CHUNK:], ALU.add
+        )
         sin_ph = held.tile([D, N], F32, name="sin_ph")
         nc.scalar.activation(sin_ph[:], rel_sb[:], FUNC.Sin, scale=PHASE_PER_REL)
         minus_sin = held.tile([D, N], F32, name="minus_sin")
@@ -184,8 +177,17 @@ def tile_rotate_kernel(tc, ent, rel, offs, out):
         cos_ph = held.tile([D, N], F32, name="cos_ph")
         nc.scalar.activation(cos_ph[:], abs_rel[:], FUNC.Sin, bias=half_pi[:], scale=-PHASE_PER_REL)
         early_rest = held.tile([128, 3 * CHUNK], F32, name="early_rest")
-        high_and_middle(early_values, early_rest, early_slots, CHUNK, nc.scalar.copy)
+        split(early_values, early_rest, early_slots, CHUNK)
         repeats(early_slots, CHUNK, nc.scalar.copy)
+        collect_early(0)
+        table_sq = held.tile([D, 2 * S], F32, name="table_sq")
+        for x, part in enumerate((re_ent, im_ent)):
+            nc.scalar.activation(
+                table_sq[:, x * S : (x + 1) * S], part[:], FUNC.Square, scale=GUARD_ROOT
+            )
+        nc.gpsimd.tensor_tensor(
+            table_values[:, 2 * S :], table_sq[:, 0:S], table_sq[:, S:], ALU.add
+        )
 
         from_re = held.tile([D, 2 * N], F32, name="from_re")
         from_im = held.tile([D, 2 * N], F32, name="from_im")
@@ -193,8 +195,6 @@ def tile_rotate_kernel(tc, ent, rel, offs, out):
         nc.vector.tensor_tensor(from_im[:, 0:N], im_ent[:].indirect(offsets[:]), minus_sin[:], ALU.mult)
         nc.vector.tensor_tensor(from_re[:, N:], re_ent[:].indirect(offsets[:]), sin_ph[:], ALU.mult)
         nc.vector.tensor_tensor(from_im[:, N:], im_ent[:].indirect(offsets[:]), cos_ph[:], ALU.mult)
-        low(early_rest, early_slots, CHUNK)
-        collect_early(0)
         rot = held.tile([D, 2 * N], F32, name="rot")
         nc.vector.tensor_tensor(rot[:], from_re[:], from_im[:], ALU.add)
 
@@ -264,11 +264,8 @@ def tile_rotate_kernel(tc, ent, rel, offs, out):
 
         make_weights(first_rows[:], 0, 1)
         make_weights(query_rows[:, N : APART * N], 1, APART - 1)
-        table_sq = enlarged_squares(table_values, S, "table_sq")
-        add_squares(table_values, table_sq, S)
         table_rest = held.tile([D, 3 * S], F32, name="table_rest")
-        high_and_middle(table_values, table_rest, table_slots, S, nc.vector.tensor_copy)
-        low(table_rest, table_slots, S)
+        split(table_values, table_rest, table_slots, S)
         repeats(table_slots, S, nc.vector.tensor_copy)
 
         def prepare(first):
@@ -346,7 +343,7 @@ def tile_rotate_kernel(tc, ent, rel, offs, out):
             if step >= AHEAD:
                 t, g = order[step - AHEAD]
                 d = set_start(t) + APART * g
-                if (step - AHEAD) % SPARED == SPARED // 2 and step - AHEAD < count - GROUPS:
+                if (step - AHEAD) % SPARED == SPARED // 2 and step - AHEAD < count - 3 * GROUPS:
                     spared_modulus = spared.tile([N, S], F32, name="spared_modulus")
                     nc.scalar.activation(
                         spared_modulus[:],

@@ -66,6 +66,7 @@ def tile_rotate_kernel(tc, ent, rel, offs, out):
     nc = tc.nc
     with (
         tc.tile_pool(name="held", bufs=1) as held,
+        tc.tile_pool(name="in_turn", bufs=1) as in_turn,
         tc.tile_pool(name="work", bufs=AHEAD + 1) as work,
         tc.tile_pool(name="spared", bufs=6) as spared,
         tc.tile_pool(name="root_work", bufs=1) as root_work,
@@ -118,9 +119,6 @@ def tile_rotate_kernel(tc, ent, rel, offs, out):
                 pattern=[[-SLOTS, GROUPS]],
                 channel_multiplier=1,
             )
-        table_values = held.tile([D, 3 * S], F32, name="table_values")
-        for x in range(2):
-            nc.gpsimd.dma_start(table_values[:, x * S : (x + 1) * S], ent[x * D : (x + 1) * D, :])
         identity_bf = held.tile([N, N], BF16, name="identity_bf")
         make_identity(nc, identity_bf[:])
 
@@ -185,31 +183,29 @@ def tile_rotate_kernel(tc, ent, rel, offs, out):
             nc.scalar.activation(
                 table_sq[:, x * S : (x + 1) * S], part[:], FUNC.Square, scale=GUARD_ROOT
             )
-        nc.gpsimd.tensor_tensor(
-            table_values[:, 2 * S :], table_sq[:, 0:S], table_sq[:, S:], ALU.add
-        )
 
-        from_re = held.tile([D, 2 * N], F32, name="from_re")
-        from_im = held.tile([D, 2 * N], F32, name="from_im")
+        rotation = in_turn.tile([D, 3 * S], F32, name="rotation", tag="in_turn")
+        from_re, from_im, rot, query_rest, rot_sq = [
+            rotation[:, 2 * N * x : 2 * N * (x + 1)] for x in range(5)
+        ]
+        rot_norm = rotation[:, 10 * N : 11 * N]
         nc.vector.tensor_tensor(from_re[:, 0:N], re_ent[:].indirect(offsets[:]), cos_ph[:], ALU.mult)
         nc.vector.tensor_tensor(from_im[:, 0:N], im_ent[:].indirect(offsets[:]), minus_sin[:], ALU.mult)
         nc.vector.tensor_tensor(from_re[:, N:], re_ent[:].indirect(offsets[:]), sin_ph[:], ALU.mult)
         nc.vector.tensor_tensor(from_im[:, N:], im_ent[:].indirect(offsets[:]), cos_ph[:], ALU.mult)
-        rot = held.tile([D, 2 * N], F32, name="rot")
-        nc.vector.tensor_tensor(rot[:], from_re[:], from_im[:], ALU.add)
+        nc.vector.tensor_tensor(rot, from_re, from_im, ALU.add)
 
         homes = [[3 * b for b in range(3)], [], []]
         for i, (a, b) in enumerate(REPEATS):
             homes[a].append(REPEAT_SLOT + 2 * i)
-        query_rest = held.tile([D, 2 * N], F32, name="query_rest")
-        nc.vector.tensor_tensor(pair(query_slots, N, homes[0][0]), from_re[:], from_im[:], ALU.add)
+        nc.vector.tensor_tensor(pair(query_slots, N, homes[0][0]), from_re, from_im, ALU.add)
         nc.vector.tensor_tensor(
-            query_rest[:], rot[:], pair(query_slots, N, homes[0][0]), ALU.subtract
+            query_rest, rot, pair(query_slots, N, homes[0][0]), ALU.subtract
         )
-        nc.vector.tensor_copy(pair(query_slots, N, homes[1][0]), query_rest[:])
+        nc.vector.tensor_copy(pair(query_slots, N, homes[1][0]), query_rest)
         nc.vector.tensor_tensor(
             pair(query_slots, N, homes[2][0]),
-            query_rest[:],
+            query_rest,
             pair(query_slots, N, homes[1][0]),
             ALU.subtract,
         )
@@ -230,17 +226,15 @@ def tile_rotate_kernel(tc, ent, rel, offs, out):
                 stop=(k == by_piece[-1]),
             )
 
-        rot_sq = held.tile([D, 2 * N], F32, name="rot_sq")
-        nc.scalar.activation(rot_sq[:], rot[:], FUNC.Square, scale=GUARD_ROOT)
+        nc.scalar.activation(rot_sq, rot, FUNC.Square, scale=GUARD_ROOT)
         warm_up_root = held.tile([D, 1], F32, name="warm_up_root")
         nc.scalar.activation(warm_up_root[:], rot_sq[:, 0:1], FUNC.Sqrt)
         for slots_of_piece in homes:
             for k in slots_of_piece[1:]:
                 nc.vector.tensor_copy(pair(query_slots, N, k), pair(query_slots, N, slots_of_piece[0]))
-        rot_norm = held.tile([D, N], F32, name="rot_norm")
-        nc.vector.tensor_tensor(rot_norm[:], rot_sq[:, 0:N], rot_sq[:, N : 2 * N], ALU.add)
+        nc.vector.tensor_tensor(rot_norm, rot_sq[:, 0:N], rot_sq[:, N : 2 * N], ALU.add)
         rot_norm_ps = vector_banks.tile([N, D], F32, name="rot_norm_ps", tag="vector_product")
-        nc.tensor.transpose(rot_norm_ps[:], rot_norm[:], identity[:])
+        nc.tensor.transpose(rot_norm_ps[:], rot_norm, identity[:])
         rot_norm_t = held.tile([N, D], F32, name="rot_norm_t")
         nc.scalar.copy(rot_norm_t[:], rot_norm_ps[:])
         collect_early(1)
@@ -264,6 +258,14 @@ def tile_rotate_kernel(tc, ent, rel, offs, out):
 
         make_weights(first_rows[:], 0, 1)
         make_weights(query_rows[:, N : APART * N], 1, APART - 1)
+        table_values = in_turn.tile([D, 3 * S], F32, name="table_values", tag="in_turn")
+        nc.scalar.dma_start(
+            table_values[:, 0 : 2 * S].rearrange("d (x s) -> d x s", x=2),
+            ent.rearrange("(x d) s -> d x s", x=2),
+        )
+        nc.vector.tensor_tensor(
+            table_values[:, 2 * S :], table_sq[:, 0:S], table_sq[:, S:], ALU.add
+        )
         table_rest = held.tile([D, 3 * S], F32, name="table_rest")
         split(table_values, table_rest, table_slots, S)
         repeats(table_slots, S, nc.vector.tensor_copy)

import math

import concourse.mybir as mybir
from concourse.masks import make_identity

F32 = mybir.dt.float32
BF16 = mybir.dt.bfloat16
U16 = mybir.dt.uint16
I32 = mybir.dt.int32
ALU = mybir.AluOpType
FUNC = mybir.ActivationFunctionType

D = 128
S = 512
N = 128
GAMMA = 12.0
PHASE_PER_REL = math.pi / 0.028

REPEATS = [(1, 0), (2, 0), (1, 1)]
REPEAT_SLOT = 9
SLOTS = 16
GROUPS = 128 // SLOTS
SETS = D // GROUPS

APART = 4
SPAN = APART * GROUPS

PARTS = 128 // SPAN
CHUNK = S // PARTS


def set_start(t):
    return SPAN * (t // APART) + t % APART


GUARD_ROOT = 1.0 + 2.0**-19

AHEAD = 4

PAIR = 2
VECTOR_SETS = range(2, SETS - 3, 2)

SPARED = 8

SIGMA = 1 - (1 + math.log(math.log(2))) / math.log(2)
SEED = 1.5 * (127 - SIGMA) * 2.0**23
U_LOW, U_HIGH = 0.8708, 0.9872


def inverse_root_polynomial(low, high):
    u = [(low + high) / 2 + (high - low) / 2 * math.cos(math.pi * (2 * k + 1) / 6) for k in range(3)]
    f = [v**-0.5 for v in u]
    slope = (f[1] - f[0]) / (u[1] - u[0])
    c2 = ((f[2] - f[1]) / (u[2] - u[1]) - slope) / (u[2] - u[0])
    c1 = slope - c2 * (u[0] + u[1])
    return f[0] - u[0] * (c1 + c2 * u[0]), c1, c2


C0, C1, C2 = inverse_root_polynomial(U_LOW, U_HIGH)
A = C2 ** (1 / 3)

FLOPS = 7 * D * N * S


def tile_rotate_kernel(tc, ent, rel, offs, out):
    nc = tc.nc
    with (
        tc.tile_pool(name="held", bufs=1) as held,
        tc.tile_pool(name="in_turn", bufs=1) as in_turn,
        tc.tile_pool(name="work", bufs=AHEAD + 1) as work,
        tc.tile_pool(name="spared", bufs=6) as spared,
        tc.tile_pool(name="root_work", bufs=1) as root_work,
        tc.psum_pool(name="banks", bufs=AHEAD + 1) as banks,
        tc.psum_pool(name="vector_banks", bufs=PAIR) as vector_banks,
        tc.psum_pool(name="once", bufs=1) as once,
    ):
        early_values = held.tile([128, 3 * CHUNK], F32, name="early_values")
        nc.sync.dma_start(
            early_values[:, 0 : 2 * CHUNK].rearrange("p (x y) -> p x y", x=2),
            ent.rearrange("(x d) (c y) -> x d c y", x=2, y=CHUNK)[:, 0:SPAN].rearrange(
                "x d c y -> (d c) x y"
            ),
        )
        rel_sb = held.tile([D, N], F32, name="rel_sb")
        nc.scalar.dma_start(rel_sb[:], rel)
        im_ent = held.tile([D, S], F32, name="im_ent")
        nc.scalar.dma_start(im_ent[:], ent[D : 2 * D, :])
        offsets = held.tile([128, N // 16], U16, name="offsets")
        nc.sync.dma_start(offsets[:], offs)
        re_ent = held.tile([D, S], F32, name="re_ent")
        nc.sync.dma_start(re_ent[:], ent[0:D, :])

        half_pi = held.tile([D, 1], F32, name="half_pi")
        nc.vector.memset(half_pi[:], math.pi / 2)
        warm_up = held.tile([D, 1], F32, name="warm_up")
        nc.scalar.activation(warm_up[:], half_pi[:], FUNC.Sin)
        query_slots = held.tile([D, SLOTS * N], BF16, name="query_slots")
        early_slots = held.tile([128, SLOTS * CHUNK], BF16, name="early_slots")
        table_slots = held.tile([D, SLOTS * S], BF16, name="table_slots")
        for b in range(3):
            nc.gpsimd.memset(query_slots[:, (3 * b + 2) * N : (3 * b + 3) * N], -0.5)
        nc.gpsimd.memset(query_slots[:, (SLOTS - 1) * N :], 0.0)
        nc.gpsimd.memset(early_slots[:, (SLOTS - 1) * CHUNK :], 0.0)
        nc.gpsimd.memset(table_slots[:, (SLOTS - 1) * S :], 0.0)
        identity = held.tile([D, D], F32, name="identity")
        make_identity(nc, identity[:])
        pick = held.tile([D, 128 + SLOTS], BF16, name="pick")
        nc.gpsimd.memset(pick[:], 0.0)
        nc.gpsimd.tensor_copy(pick[:, SLOTS - 1 : 128 : SLOTS], identity[:, 0:SPAN:APART])
        own_group = held.tile([128, GROUPS], F32, name="own_group")
        nc.gpsimd.memset(own_group[:], 0.0)
        for compare, fill, base in ((ALU.is_gt, -2.0, 1 - SLOTS), (ALU.is_ge, 0.0, 0)):
            nc.gpsimd.affine_select(
                out=own_group[:],
                in_=own_group[:],
                compare_op=compare,
                fill=fill,
                base=base,
                pattern=[[-SLOTS, GROUPS]],
                channel_multiplier=1,
            )
        identity_bf = held.tile([N, N], BF16, name="identity_bf")
        make_identity(nc, identity_bf[:])

        query_rows = held.tile([128, SETS * N], BF16, name="query_rows")
        table_rows = held.tile([128, SETS * S], BF16, name="table_rows")

        def collect(rows, slots, width, t):
            last = set_start(t) + APART * (GROUPS - 1)
            nc.sync.dma_start(
                rows[:, t * width : (t + 1) * width], slots[set_start(t) : last + 1 : APART, :]
            )

        def collect_early(t):
            for c in range(PARTS):
                first = PARTS * set_start(t) + c
                last = first + PARTS * APART * (GROUPS - 1)
                queue = nc.scalar if t == 0 and c % 2 == 1 else nc.sync
                queue.dma_start(
                    table_rows[:, t * S + c * CHUNK : t * S + (c + 1) * CHUNK],
                    early_slots[first : last + 1 : PARTS * APART, :],
                )

        def piece(slots, width, b):
            return slots[:, 3 * b * width : 3 * (b + 1) * width]

        def pair(slots, width, k):
            return slots[:, k * width : (k + 2) * width]

        def split(values, rest, slots, width):
            nc.vector.tensor_copy(piece(slots, width, 0), values[:])
            nc.vector.tensor_tensor(rest[:], values[:], piece(slots, width, 0), ALU.subtract)
            nc.vector.tensor_copy(piece(slots, width, 1), rest[:])
            nc.vector.tensor_tensor(
                piece(slots, width, 2), rest[:], piece(slots, width, 1), ALU.subtract
            )

        def repeats(slots, width, copy):
            for i, (a, b) in enumerate(REPEATS):
                copy(pair(slots, width, REPEAT_SLOT + 2 * i), pair(slots, width, 3 * b))

        early_sq = held.tile([128, 2 * CHUNK], F32, name="early_sq")
        nc.scalar.activation(
            early_sq[:], early_values[:, 0 : 2 * CHUNK], FUNC.Square, scale=GUARD_ROOT
        )
        nc.vector.tensor_tensor(
            early_values[:, 2 * CHUNK :], early_sq[:, 0:CHUNK], early_sq[:, CHUNK:], ALU.add
        )
        sin_ph = held.tile([D, N], F32, name="sin_ph")
        nc.scalar.activation(sin_ph[:], rel_sb[:], FUNC.Sin, scale=PHASE_PER_REL)
        minus_sin = held.tile([D, N], F32, name="minus_sin")
        nc.scalar.activation(minus_sin[:], rel_sb[:], FUNC.Sin, scale=-PHASE_PER_REL)
        abs_rel = held.tile([D, N], F32, name="abs_rel")
        nc.scalar.activation(abs_rel[:], rel_sb[:], FUNC.Abs)
        cos_ph = held.tile([D, N], F32, name="cos_ph")
        nc.scalar.activation(cos_ph[:], abs_rel[:], FUNC.Sin, bias=half_pi[:], scale=-PHASE_PER_REL)
        early_rest = held.tile([128, 3 * CHUNK], F32, name="early_rest")
        split(early_values, early_rest, early_slots, CHUNK)
        repeats(early_slots, CHUNK, nc.scalar.copy)
        collect_early(0)
        table_sq = held.tile([D, 2 * S], F32, name="table_sq")
        for x, part in enumerate((re_ent, im_ent)):
            nc.scalar.activation(
                table_sq[:, x * S : (x + 1) * S], part[:], FUNC.Square, scale=GUARD_ROOT
            )

        rotation = in_turn.tile([D, 3 * S], F32, name="rotation", tag="in_turn")
        from_re, from_im, rot, query_rest, rot_sq = [
            rotation[:, 2 * N * x : 2 * N * (x + 1)] for x in range(5)
        ]
        rot_norm = rotation[:, 10 * N : 11 * N]
        nc.vector.tensor_tensor(from_re[:, 0:N], re_ent[:].indirect(offsets[:]), cos_ph[:], ALU.mult)
        nc.vector.tensor_tensor(from_im[:, 0:N], im_ent[:].indirect(offsets[:]), minus_sin[:], ALU.mult)
        nc.vector.tensor_tensor(from_re[:, N:], re_ent[:].indirect(offsets[:]), sin_ph[:], ALU.mult)
        nc.vector.tensor_tensor(from_im[:, N:], im_ent[:].indirect(offsets[:]), cos_ph[:], ALU.mult)
        nc.vector.tensor_tensor(rot, from_re, from_im, ALU.add)

        homes = [[3 * b for b in range(3)], [], []]
        for i, (a, b) in enumerate(REPEATS):
            homes[a].append(REPEAT_SLOT + 2 * i)
        nc.vector.tensor_tensor(pair(query_slots, N, homes[0][0]), from_re, from_im, ALU.add)
        nc.vector.tensor_tensor(
            query_rest, rot, pair(query_slots, N, homes[0][0]), ALU.subtract
        )
        nc.vector.tensor_copy(pair(query_slots, N, homes[1][0]), query_rest)
        nc.vector.tensor_tensor(
            pair(query_slots, N, homes[2][0]),
            query_rest,
            pair(query_slots, N, homes[1][0]),
            ALU.subtract,
        )

        source = list(range(SLOTS - 1))
        for slots_of_piece in homes:
            for k in slots_of_piece[1:]:
                for x in range(2):
                    source[k + x] = slots_of_piece[0] + x
        by_piece = sorted(range(SLOTS - 1), key=lambda k: source[k])
        first_rows = vector_banks.tile([128, N], F32, name="first_rows", tag="vector_product")
        for k in by_piece:
            nc.tensor.matmul(
                first_rows[:],
                pick[:, SLOTS - 1 - k : SLOTS - 1 - k + 128],
                query_slots[:, source[k] * N : (source[k] + 1) * N],
                start=(k == by_piece[0]),
                stop=(k == by_piece[-1]),
            )

        nc.scalar.activation(rot_sq, rot, FUNC.Square, scale=GUARD_ROOT)
        warm_up_root = held.tile([D, 1], F32, name="warm_up_root")
        nc.scalar.activation(warm_up_root[:], rot_sq[:, 0:1], FUNC.Sqrt)
        for slots_of_piece in homes:
            for k in slots_of_piece[1:]:
                nc.vector.tensor_copy(pair(query_slots, N, k), pair(query_slots, N, slots_of_piece[0]))
        nc.vector.tensor_tensor(rot_norm, rot_sq[:, 0:N], rot_sq[:, N : 2 * N], ALU.add)
        rot_norm_ps = vector_banks.tile([N, D], F32, name="rot_norm_ps", tag="vector_product")
        nc.tensor.transpose(rot_norm_ps[:], rot_norm, identity[:])
        rot_norm_t = held.tile([N, D], F32, name="rot_norm_t")
        nc.scalar.copy(rot_norm_t[:], rot_norm_ps[:])
        collect_early(1)
        for t in range(1, APART):
            collect(query_rows, query_slots, N, t)
        for t in range(2, APART):
            collect_early(t)

        weights = held.tile([128, D * N], BF16, name="weights")

        def make_weights(rows, t, count):
            for g in range(GROUPS):
                d = set_start(t) + APART * g
                nc.vector.tensor_scalar(
                    weights[:, d * N : (d + count) * N],
                    rows,
                    own_group[:, g : g + 1],
                    None,
                    ALU.mult,
                )

        make_weights(first_rows[:], 0, 1)
        make_weights(query_rows[:, N : APART * N], 1, APART - 1)
        table_values = in_turn.tile([D, 3 * S], F32, name="table_values", tag="in_turn")
        nc.scalar.dma_start(
            table_values[:, 0 : 2 * S].rearrange("d (x s) -> d x s", x=2),
            ent.rearrange("(x d) s -> d x s", x=2),
        )
        nc.vector.tensor_tensor(
            table_values[:, 2 * S :], table_sq[:, 0:S], table_sq[:, S:], ALU.add
        )
        table_rest = held.tile([D, 3 * S], F32, name="table_rest")
        split(table_values, table_rest, table_slots, S)
        repeats(table_slots, S, nc.vector.tensor_copy)

        def prepare(first):
            for t in range(first, first + APART):
                collect(query_rows, query_slots, N, t)
            for t in range(first, first + APART):
                collect(table_rows, table_slots, S, t)
            make_weights(query_rows[:, first * N : (first + APART) * N], first, APART)

        prepare(APART)

        vector_sum = held.tile([N, PAIR * S], F32, name="vector_sum")
        nc.gpsimd.memset(vector_sum[:, 0:S], -GAMMA)
        nc.gpsimd.memset(vector_sum[:, S:], 0.0)
        vector_total = held.tile([N, S], F32, name="vector_total")

        def vector_roots(t):
            wide = [N, PAIR * S]
            value = root_work.tile(wide, F32, name="value")
            for i in range(PAIR):
                d = set_start(t) + APART * i
                product = vector_banks.tile([N, S], F32, name="product", tag="vector_product")
                nc.tensor.matmul(
                    product[:],
                    weights[:, d * N : (d + 1) * N],
                    table_rows[:, t * S : (t + 1) * S],
                    start=True,
                    stop=True,
                )
                nc.vector.tensor_scalar(
                    value[:, i * S : (i + 1) * S], product[:], rot_norm_t[:, d : d + 1], None, ALU.add
                )
            seed = root_work.tile(wide, I32, name="seed")
            nc.vector.tensor_scalar(seed[:], value[:].bitcast(I32), -0.5, SEED, ALU.mult, ALU.add)
            guess = seed[:].bitcast(F32)
            a = root_work.tile(wide, F32, name="a")
            nc.vector.scalar_tensor_tensor(a[:], value[:], A, guess, ALU.mult, ALU.mult)
            b = root_work.tile(wide, F32, name="b")
            nc.vector.tensor_tensor(b[:], a[:], guess, ALU.mult)
            parabola = root_work.tile(wide, F32, name="parabola")
            nc.vector.scalar_tensor_tensor(parabola[:], b[:], C1 / A**2, b[:], ALU.add, ALU.mult)
            vector_modulus = root_work.tile(wide, F32, name="vector_modulus")
            nc.vector.scalar_tensor_tensor(
                vector_modulus[:], parabola[:], C0 / A, a[:], ALU.add, ALU.mult
            )
            nc.vector.tensor_tensor(vector_sum[:], vector_sum[:], vector_modulus[:], ALU.add)

        order = [
            (t, g)
            for t in range(SETS)
            for g in range(GROUPS)
            if not (t in VECTOR_SETS and g < PAIR)
        ]
        count = len(order)
        dist_sum = once.tile([N, S], F32, name="dist_sum")
        products = []
        for step in range(count + AHEAD):
            if step < count:
                t, g = order[step]
                d = set_start(t) + APART * g
                if t in VECTOR_SETS and g == PAIR:
                    vector_roots(t)
                    missing = APART * (VECTOR_SETS.index(t) + 2)
                    if missing < SETS:
                        prepare(missing)
                mod_sq = banks.tile([N, S], F32, name="mod_sq")
                nc.tensor.matmul(
                    mod_sq[:],
                    weights[:, d * N : (d + 1) * N],
                    table_rows[:, t * S : (t + 1) * S],
                    start=True,
                    stop=True,
                )
                products.append(mod_sq)
            if step >= AHEAD:
                t, g = order[step - AHEAD]
                d = set_start(t) + APART * g
                if (step - AHEAD) % SPARED == SPARED // 2 and step - AHEAD < count - 3 * GROUPS:
                    spared_modulus = spared.tile([N, S], F32, name="spared_modulus")
                    nc.scalar.activation(
                        spared_modulus[:],
                        products[step - AHEAD][:],
                        FUNC.Sqrt,
                        bias=rot_norm_t[:, d : d + 1],
                    )
                    nc.vector.tensor_tensor(
                        vector_sum[:, 0:S], vector_sum[:, 0:S], spared_modulus[:], ALU.add
                    )
                else:
                    modulus = work.tile([N, S], BF16, name="modulus")
                    nc.scalar.activation(
                        modulus[:], products[step - AHEAD][:], FUNC.Sqrt, bias=rot_norm_t[:, d : d + 1]
                    )
                    nc.tensor.matmul(
                        dist_sum[:],
                        identity_bf[:],
                        modulus[:],
                        start=(step == AHEAD),
                        stop=(step == count + AHEAD - 1),
                    )

        nc.vector.tensor_tensor(vector_total[:], vector_sum[:, 0:S], vector_sum[:, S:], ALU.add)
        score = held.tile([N, S], F32, name="score")
        nc.vector.scalar_tensor_tensor(
            score[:], dist_sum[:], -1.0, vector_total[:], ALU.mult, ALU.subtract
        )
        nc.sync.dma_start(out, score[:])
